import numpy as np
import ml_dtypes


def mxq(x, axis, fmt="e4m3"):
    dtype, down = {"e4m3": (ml_dtypes.float8_e4m3fn, 7), "e5m2": (ml_dtypes.float8_e5m2, 14)}[fmt]
    v = np.moveaxis(np.asarray(x, np.float32).astype(ml_dtypes.bfloat16).astype(np.float64), axis, -1)
    blocks = v.reshape(v.shape[:-1] + (-1, 32))
    amax = np.abs(blocks).max(-1, keepdims=True)
    byte = np.maximum(np.where(amax > 0, np.frexp(amax)[1] - 1 + 127, 0) - down, 1)
    scale = np.exp2(byte - 127.0)
    codes = (blocks / scale).astype(np.float32).astype(dtype).astype(np.float64)
    return np.moveaxis((codes * scale).reshape(v.shape), -1, axis)


WIDE = False


def mx_kscale(k):
    if not WIDE:
        return np.ones(k)
    levels = np.array([10, -10, 5, -5, 0])
    if k % 512:
        return np.exp2(np.random.permutation(np.resize(levels, k // 32))).repeat(32)
    a = np.empty((k // 512, 16))
    for p in range(k // 512):
        a[p, :8] = np.random.permutation(np.resize(levels, 8))
        for g in range(8):
            far = levels[np.abs(levels - a[p, g]) >= 10]
            a[p, g + 8] = far[np.random.randint(len(far))]
    return np.exp2(a.ravel()).repeat(32)


BF16 = ml_dtypes.bfloat16


def bf(x):
    return np.asarray(x, np.float32).astype(BF16)


def f64(x):
    return np.asarray(x).astype(np.float64)


B, D, R = 2048, 2048, 128


def softplus(v):
    return np.log1p(np.exp(v))


def setup_inputs():
    s = mx_kscale(D)
    w = 1.0 / np.sqrt(D)
    return {"x": bf(np.random.standard_normal((B, D)) * s),
            "state_re": bf(np.random.standard_normal((B, R))),
            "state_im": bf(np.random.standard_normal((B, R))),
            "W_dt": bf(np.random.standard_normal((R, D)) * 0.5 * w / s),
            "b_dt": bf(np.random.standard_normal(R) * 0.3),
            "W_ph": bf(np.random.standard_normal((R, D)) * 0.5 * w / s),
            "b_ph": bf(np.random.standard_normal(R) * 0.3),
            "W_B": bf(np.random.standard_normal((R, D)) * w / s),
            "A_real": bf(np.random.standard_normal(R) * 0.5),
            "A_imag": bf(np.random.standard_normal(R) * 0.5)}


def reference(x, state_re, state_im, W_dt, b_dt, W_ph, b_ph, W_B, A_real, A_imag):
    xq = mxq(f64(x), 1, "e4m3")
    dt = softplus((xq @ mxq(f64(W_dt), 1, "e4m3").T) + f64(b_dt))
    phase = np.tanh((xq @ mxq(f64(W_ph), 1, "e4m3").T) + f64(b_ph)) * np.pi
    decay = np.exp(-dt * np.exp(f64(A_real)))
    angle = dt * f64(A_imag) + phase
    B_val = xq @ mxq(f64(W_B), 1, "e4m3").T
    cos = np.cos(angle)
    sin = np.sin(angle)
    new_re = (f64(state_re) * cos - f64(state_im) * sin) * decay + B_val
    new_im = (f64(state_re) * sin + f64(state_im) * cos) * decay
    return new_re, new_im

@@ -1,0 +1,318 @@
+import math
+from contextlib import ExitStack
+
+import concourse.mybir as mybir
+from concourse.masks import make_identity
+
+F32 = mybir.dt.float32
+BF16 = mybir.dt.bfloat16
+U32 = mybir.dt.uint32
+U8 = mybir.dt.uint8
+FP8X4 = mybir.dt.float8_e4m3fn_x4
+ACT = mybir.ActivationFunctionType
+ALU = mybir.AluOpType
+
+B, D, R = 2048, 2048, 128
+FLOPS = 2 * B * D * 3 * R
+
+P = 128
+PACK = 4
+K_PASS = P * PACK
+PASSES = D // K_PASS
+WORDS_PASS = K_PASS // 2
+
+ROW_TILES = B // P
+PIECE_TILES = 2
+PIECES = ROW_TILES // PIECE_TILES
+PIECE_COLS = PIECE_TILES * P
+CHUNK_TILES = 4
+CHUNK_COLS = CHUNK_TILES * P
+CHUNKS = ROW_TILES // CHUNK_TILES
+PIECES_PER_CHUNK = CHUNK_TILES // PIECE_TILES
+
+X_BUFFERS = 6
+PRODUCT_LAG = 2
+PSUM_BANKS = 8
+ABREAST = 2
+SCALAR_BANKS = 3
+
+ROUND_MAGIC = 1.5 * 2.0**23
+EXP_CAP = 2.0**60
+
+
+def tile_mamba3mimoblock_pa_kernel(
+    tc, x, state_re, state_im, W_dt, b_dt, W_ph, b_ph, W_B, A_real, A_imag, out_0, out_1
+):
+    nc = tc.nc
+    with ExitStack() as ctx:
+        const = ctx.enter_context(tc.tile_pool(name="const", bufs=1))
+        xpool = ctx.enter_context(tc.tile_pool(name="xpool", bufs=X_BUFFERS))
+        stage = ctx.enter_context(tc.tile_pool(name="stage", bufs=3))
+        keep = ctx.enter_context(tc.tile_pool(name="keep", bufs=1))
+        chan = ctx.enter_context(tc.tile_pool(name="chan", bufs=CHUNKS))
+        rows = ctx.enter_context(tc.tile_pool(name="rows", bufs=CHUNKS))
+        psum = ctx.enter_context(tc.psum_pool(name="psum", bufs=PSUM_BANKS))
+        ctx.enter_context(tc.manual_schedule())
+
+        x_rows = x.rearrange("(p t) k -> p t k", t=ROW_TILES)
+        re_rows = out_0.rearrange("(p t) r -> p t r", t=ROW_TILES)
+        im_rows = out_1.rearrange("(p t) r -> p t r", t=ROW_TILES)
+
+        vec_rows = const.tile([P, P], BF16)
+        nc.vector.memset(vec_rows[:], 0.0)
+        for i, vec in enumerate((b_dt, b_ph, A_real, A_imag)):
+            nc.scalar.dma_start(out=vec_rows[i : i + 1, :], in_=vec.rearrange("(o r) -> o r", o=1))
+
+        w_sb = const.tile([P, 3, D], BF16)
+        nc.sync.dma_start(out=w_sb[:, 0, :], in_=W_dt)
+        nc.sync.dma_start(out=w_sb[:, 1, :], in_=W_ph)
+        x_sb = []
+        for piece in range(PIECES):
+            x_piece = xpool.tile([P, PIECE_TILES, D], BF16)
+            t0 = piece * PIECE_TILES
+            nc.sync.dma_start(out=x_piece[:], in_=x_rows[:, t0 : t0 + PIECE_TILES, :])
+            x_sb.append(x_piece)
+        nc.sync.dma_start(out=w_sb[:, 2, :], in_=W_B)
+        st_re = const.tile([P, ROW_TILES, R], BF16)
+        st_im = const.tile([P, ROW_TILES, R], BF16)
+        nc.sync.dma_start(out=st_re[:], in_=state_re.rearrange("(p t) r -> p t r", t=ROW_TILES))
+        nc.sync.dma_start(out=st_im[:], in_=state_im.rearrange("(p t) r -> p t r", t=ROW_TILES))
+
+        ident = const.tile([P, P], F32)
+        make_identity(nc, ident[:])
+
+        def transposes_and_copies(words, n_tiles, scalar_banks):
+            grouped = stage.tile([P, PASSES * n_tiles * P * PACK], BF16, tag="grouped", align_bytes=64)
+            grouped_words = grouped[:].bitcast(F32).rearrange("q (g c u) -> q g c u", g=PASSES, u=2)
+            for g in range(PASSES):
+                bank = psum.tile([P, 2, n_tiles, P], F32, tag="bank")
+                for u in range(2):
+                    w0 = g * WORDS_PASS + u
+                    for j in range(n_tiles):
+                        nc.tensor.transpose(
+                            bank[:, u, j, :], words[:, j, w0 : (g + 1) * WORDS_PASS : 2], ident[:]
+                        )
+                halves = bank[:].rearrange("q u j p -> q (j p) u")
+                if g < scalar_banks:
+                    nc.scalar.copy(out=grouped_words[:, g], in_=halves)
+                else:
+                    nc.vector.tensor_copy(out=grouped_words[:, g], in_=halves)
+            return grouped
+
+        w_words = w_sb[:].bitcast(F32)
+        w2_codes = keep.tile([P, PASSES, 2, P], U32, align_bytes=64)
+        w2_scales = keep.tile([P, PASSES, 2, P], U8, align_bytes=64)
+        wb_codes = keep.tile([P, PASSES, P], U32, align_bytes=64)
+        wb_scales = keep.tile([P, PASSES, P], U8, align_bytes=64)
+        w2_grouped = transposes_and_copies(w_words[:, 0:2, :], 2, 2)
+        nc.vector.quantize_mx(
+            out=w2_codes[:].rearrange("q g j r -> q (g j r)").bitcast(FP8X4),
+            scales=w2_scales[:].rearrange("q g j r -> q (g j r)"),
+            in_=w2_grouped[:],
+        )
+
+        vec_f32 = const.tile([P, P], F32)
+        nc.vector.tensor_copy(out=vec_f32[:], in_=vec_rows[:])
+        vec_t = psum.tile([P, P], F32, tag="bank")
+        nc.tensor.transpose(vec_t[:], vec_f32[:], ident[:])
+        per_chan = const.tile([P, 4], F32)
+        nc.vector.tensor_copy(out=per_chan[:], in_=vec_t[:, 0:4])
+        b_dt_col = per_chan[:, 0:1]
+        b_ph_col = per_chan[:, 1:2]
+        a_col = const.tile([P, 1], F32)
+        nc.scalar.activation(out=a_col[:], in_=per_chan[:, 2:3], func=ACT.Exp)
+        neg_a_col = const.tile([P, 1], F32)
+        nc.vector.tensor_scalar_mul(out=neg_a_col[:], in0=a_col[:], scalar1=-1.0)
+        turns_col = const.tile([P, 1], F32)
+        nc.vector.tensor_scalar_mul(out=turns_col[:], in0=per_chan[:, 3:4], scalar1=1.0 / (2.0 * math.pi))
+
+        x_codes = keep.tile([P, PIECES, PASSES, PIECE_TILES, P], U32, align_bytes=64)
+        x_scales = keep.tile([P, PIECES, PASSES, PIECE_TILES, P], U8, align_bytes=64)
+        z_dt = {}
+        z_ph = {}
+        z_b = {}
+        soft = {}
+        turn = {}
+        frac = {}
+        sine = {}
+        cosine = {}
+        re_part = {}
+        im_part = {}
+
+        def quantise(piece, grouped):
+            nc.vector.quantize_mx(
+                out=x_codes[:, piece].rearrange("q g j p -> q (g j p)").bitcast(FP8X4),
+                scales=x_scales[:, piece].rearrange("q g j p -> q (g j p)"),
+                in_=grouped[:],
+            )
+
+        def products(piece):
+            c = piece // PIECES_PER_CHUNK
+            half = piece % PIECES_PER_CHUNK
+            if half == 0:
+                z_dt[c] = psum.tile([P, CHUNK_COLS], F32, name="z_dt", tag="bank")
+                z_ph[c] = psum.tile([P, CHUNK_COLS], F32, name="z_ph", tag="bank")
+            cols = slice(half * PIECE_COLS, (half + 1) * PIECE_COLS)
+            for i, z in enumerate((z_dt[c], z_ph[c])):
+                for g in range(PASSES):
+                    nc.tensor.matmul_mx(
+                        out=z[:, cols],
+                        lhsT=w2_codes[:, g, i, :].bitcast(FP8X4),
+                        lhsT_scale=w2_scales[:, g, i, :],
+                        rhs=x_codes[:, piece, g].rearrange("q j p -> q (j p)").bitcast(FP8X4),
+                        rhs_scale=x_scales[:, piece, g].rearrange("q j p -> q (j p)"),
+                        start=(g == 0),
+                        stop=(g == PASSES - 1),
+                    )
+
+        def exp_and_tanh(c):
+            soft[c] = chan.tile([P, CHUNK_COLS], F32, name="soft", tag="soft")
+            turn[c] = chan.tile([P, CHUNK_COLS], F32, name="turn", tag="turn")
+            nc.scalar.activation(out=soft[c][:], in_=z_dt[c][:], func=ACT.Exp, bias=b_dt_col, scale=1.0)
+            nc.scalar.activation(out=turn[c][:], in_=z_ph[c][:], func=ACT.Tanh, bias=b_ph_col, scale=1.0)
+            nc.vector.tensor_scalar_min(out=soft[c][:], in0=soft[c][:], scalar1=EXP_CAP)
+            nc.vector.tensor_scalar_mul(out=turn[c][:], in0=turn[c][:], scalar1=0.5)
+
+        def b_val(c):
+            z_b[c] = psum.tile([P, CHUNK_TILES, R], F32, name="z_b", tag="bank")
+            for jj in range(CHUNK_TILES):
+                piece = (c * CHUNK_TILES + jj) // PIECE_TILES
+                j = (c * CHUNK_TILES + jj) % PIECE_TILES
+                for g in range(PASSES):
+                    nc.tensor.matmul_mx(
+                        out=z_b[c][:, jj, :],
+                        lhsT=x_codes[:, piece, g, j, :].bitcast(FP8X4),
+                        lhsT_scale=x_scales[:, piece, g, j, :],
+                        rhs=wb_codes[:, g, :].bitcast(FP8X4),
+                        rhs_scale=wb_scales[:, g, :],
+                        start=(g == 0),
+                        stop=(g == PASSES - 1),
+                    )
+
+        def logarithm(c):
+            nc.scalar.activation(out=soft[c][:], in_=soft[c][:], func=ACT.Ln, bias=1.0, scale=1.0)
+
+        def step_size(c):
+            nc.vector.scalar_tensor_tensor(
+                out=soft[c][:], in0=z_dt[c][:], scalar=b_dt_col, in1=soft[c][:], op0=ALU.add, op1=ALU.max
+            )
+
+        def angle_in_turns(c):
+            nc.vector.scalar_tensor_tensor(
+                out=turn[c][:], in0=soft[c][:], scalar=turns_col[:], in1=turn[c][:], op0=ALU.mult, op1=ALU.add
+            )
+
+        def nearest_turn(c):
+            frac[c] = chan.tile([P, CHUNK_COLS], F32, name="frac", tag="frac")
+            nc.vector.tensor_scalar(
+                out=frac[c][:], in0=turn[c][:], scalar1=ROUND_MAGIC, scalar2=ROUND_MAGIC,
+                op0=ALU.add, op1=ALU.subtract,
+            )
+
+        def fraction(c):
+            nc.vector.tensor_sub(out=frac[c][:], in0=frac[c][:], in1=turn[c][:])
+
+        def sine_of(c):
+            sine[c] = chan.tile([P, CHUNK_COLS], F32, name="sine", tag="sine")
+            nc.scalar.activation(out=sine[c][:], in_=frac[c][:], func=ACT.Sin, scale=-2.0 * math.pi)
+
+        def magnitude_of(c):
+            cosine[c] = chan.tile([P, CHUNK_COLS], F32, name="cosine", tag="cosine")
+            nc.scalar.activation(out=cosine[c][:], in_=frac[c][:], func=ACT.Abs)
+
+        def cosine_of(c):
+            nc.scalar.activation(
+                out=cosine[c][:], in_=cosine[c][:], func=ACT.Sin, scale=-2.0 * math.pi, bias=math.pi / 2.0
+            )
+
+        def decay(c):
+            nc.scalar.activation(out=soft[c][:], in_=soft[c][:], func=ACT.Exp, scale=neg_a_col[:])
+
+        def back_to_rows(channel_tile):
+            bank = psum.tile([P, CHUNK_TILES, R], F32, name="row_bank", tag="bank")
+            for jj in range(CHUNK_TILES):
+                nc.tensor.transpose(bank[:, jj, :], channel_tile[:, jj * P : (jj + 1) * P], ident[:])
+            return bank
+
+        def rotate(c):
+            t0 = c * CHUNK_TILES
+            sr = st_re[:, t0 : t0 + CHUNK_TILES, :]
+            si = st_im[:, t0 : t0 + CHUNK_TILES, :]
+            sin_t = back_to_rows(sine[c])
+            cos_t = back_to_rows(cosine[c])
+            re_sin = rows.tile([P, CHUNK_TILES, R], F32, tag="re_sin")
+            im_sin = rows.tile([P, CHUNK_TILES, R], F32, tag="im_sin")
+            re_cos = rows.tile([P, CHUNK_TILES, R], F32, tag="re_cos")
+            im_cos = rows.tile([P, CHUNK_TILES, R], F32, tag="im_cos")
+            nc.vector.tensor_mul(out=re_sin[:], in0=sr, in1=sin_t[:])
+            nc.vector.tensor_mul(out=im_sin[:], in0=si, in1=sin_t[:])
+            nc.vector.tensor_mul(out=re_cos[:], in0=sr, in1=cos_t[:])
+            nc.vector.tensor_mul(out=im_cos[:], in0=si, in1=cos_t[:])
+            nc.gpsimd.tensor_add(out=re_sin[:], in0=re_sin[:], in1=im_cos[:])
+            nc.gpsimd.tensor_sub(out=re_cos[:], in0=re_cos[:], in1=im_sin[:])
+            im_part[c] = re_sin
+            re_part[c] = re_cos
+
+        def damp_and_store(c):
+            t0 = c * CHUNK_TILES
+            decay_t = back_to_rows(soft[c])
+            nc.vector.tensor_mul(out=re_part[c][:], in0=re_part[c][:], in1=decay_t[:])
+            nc.vector.tensor_mul(out=im_part[c][:], in0=im_part[c][:], in1=decay_t[:])
+            nc.sync.dma_start(out=im_rows[:, t0 : t0 + CHUNK_TILES, :], in_=im_part[c][:])
+            nc.vector.tensor_add(out=re_part[c][:], in0=re_part[c][:], in1=z_b[c][:])
+            nc.sync.dma_start(out=re_rows[:, t0 : t0 + CHUNK_TILES, :], in_=re_part[c][:])
+
+        def angles(abreast):
+            for c in abreast:
+                step_size(c)
+            for c in abreast:
+                angle_in_turns(c)
+            for c in abreast:
+                nearest_turn(c)
+            for c in abreast:
+                fraction(c)
+
+        first_half = range(0, CHUNKS // 2)
+        second_half = range(CHUNKS // 2, CHUNKS)
+
+        for piece in range(PIECES):
+            quantise(piece, transposes_and_copies(x_sb[piece][:].bitcast(F32), PIECE_TILES, SCALAR_BANKS))
+            behind = piece - PRODUCT_LAG
+            if 0 <= behind < PIECES // 2:
+                products(behind)
+                if behind % PIECES_PER_CHUNK == PIECES_PER_CHUNK - 1:
+                    exp_and_tanh(behind // PIECES_PER_CHUNK)
+
+        for c in first_half:
+            logarithm(c)
+        wb_grouped = transposes_and_copies(w_words[:, 2:3, :], 1, 0)
+        nc.vector.quantize_mx(
+            out=wb_codes[:].rearrange("q g r -> q (g r)").bitcast(FP8X4),
+            scales=wb_scales[:].rearrange("q g r -> q (g r)"),
+            in_=wb_grouped[:],
+        )
+        for piece in range(PIECES // 2, PIECES):
+            products(piece)
+        angles(first_half)
+        for c in second_half:
+            exp_and_tanh(c)
+        for c in range(CHUNKS):
+            b_val(c)
+        for c in second_half:
+            logarithm(c)
+        angles(second_half)
+
+        for first in range(0, CHUNKS, ABREAST):
+            abreast = range(first, first + ABREAST)
+            for c in abreast:
+                sine_of(c)
+            for c in abreast:
+                magnitude_of(c)
+            for c in abreast:
+                cosine_of(c)
+        for c in range(CHUNKS):
+            decay(c)
+        for c in range(CHUNKS):
+            rotate(c)
+        for c in range(CHUNKS):
+            damp_and_store(c)

@@ -36,6 +36,8 @@ PSUM_BANKS = 8
 ABREAST = 2
 SCALAR_BANKS = 3
 
+SORTED_PASSES = (3,)
+
 ROUND_MAGIC = 1.5 * 2.0**23
 EXP_CAP = 2.0**60
 
@@ -81,17 +83,24 @@ def tile_mamba3mimoblock_pa_kernel(
         ident = const.tile([P, P], F32)
         make_identity(nc, ident[:])
 
-        def transposes_and_copies(words, n_tiles, scalar_banks):
+        def transposes_and_copies(words, n_tiles, scalar_banks, sorted_passes):
             grouped = stage.tile([P, PASSES * n_tiles * P * PACK], BF16, tag="grouped", align_bytes=64)
             grouped_words = grouped[:].bitcast(F32).rearrange("q (g c u) -> q g c u", g=PASSES, u=2)
             for g in range(PASSES):
                 bank = psum.tile([P, 2, n_tiles, P], F32, tag="bank")
+                pass_words = words[:, :, g * WORDS_PASS : (g + 1) * WORDS_PASS]
+                if g in sorted_passes:
+                    by_parity = stage.tile([P, n_tiles, 2, P], F32, tag="by_parity")
+                    nc.gpsimd.tensor_copy(
+                        out=by_parity[:], in_=pass_words.rearrange("p j (q u) -> p j u q", u=2)
+                    )
                 for u in range(2):
-                    w0 = g * WORDS_PASS + u
                     for j in range(n_tiles):
-                        nc.tensor.transpose(
-                            bank[:, u, j, :], words[:, j, w0 : (g + 1) * WORDS_PASS : 2], ident[:]
-                        )
+                        if g in sorted_passes:
+                            chosen = by_parity[:, j, u, :]
+                        else:
+                            chosen = pass_words[:, j, u:WORDS_PASS:2]
+                        nc.tensor.transpose(bank[:, u, j, :], chosen, ident[:])
                 halves = bank[:].rearrange("q u j p -> q (j p) u")
                 if g < scalar_banks:
                     nc.scalar.copy(out=grouped_words[:, g], in_=halves)
@@ -104,7 +113,7 @@ def tile_mamba3mimoblock_pa_kernel(
         w2_scales = keep.tile([P, PASSES, 2, P], U8, align_bytes=64)
         wb_codes = keep.tile([P, PASSES, P], U32, align_bytes=64)
         wb_scales = keep.tile([P, PASSES, P], U8, align_bytes=64)
-        w2_grouped = transposes_and_copies(w_words[:, 0:2, :], 2, 2)
+        w2_grouped = transposes_and_copies(w_words[:, 0:2, :], 2, 2, ())
         nc.vector.quantize_mx(
             out=w2_codes[:].rearrange("q g j r -> q (g j r)").bitcast(FP8X4),
             scales=w2_scales[:].rearrange("q g j r -> q (g j r)"),
@@ -276,7 +285,7 @@ def tile_mamba3mimoblock_pa_kernel(
         second_half = range(CHUNKS // 2, CHUNKS)
 
         for piece in range(PIECES):
-            quantise(piece, transposes_and_copies(x_sb[piece][:].bitcast(F32), PIECE_TILES, SCALAR_BANKS))
+            quantise(piece, transposes_and_copies(x_sb[piece][:].bitcast(F32), PIECE_TILES, SCALAR_BANKS, SORTED_PASSES))
             behind = piece - PRODUCT_LAG
             if 0 <= behind < PIECES // 2:
                 products(behind)
@@ -285,7 +294,7 @@ def tile_mamba3mimoblock_pa_kernel(
 
         for c in first_half:
             logarithm(c)
-        wb_grouped = transposes_and_copies(w_words[:, 2:3, :], 1, 0)
+        wb_grouped = transposes_and_copies(w_words[:, 2:3, :], 1, 0, ())
         nc.vector.quantize_mx(
             out=wb_codes[:].rearrange("q g r -> q (g r)").bitcast(FP8X4),
             scales=wb_scales[:].rearrange("q g r -> q (g r)"),

@@ -8,6 +8,7 @@ F32 = mybir.dt.float32
 BF16 = mybir.dt.bfloat16
 U32 = mybir.dt.uint32
 U8 = mybir.dt.uint8
+I32 = mybir.dt.int32
 FP8X4 = mybir.dt.float8_e4m3fn_x4
 ACT = mybir.ActivationFunctionType
 ALU = mybir.AluOpType
@@ -31,15 +32,24 @@ CHUNKS = ROW_TILES // CHUNK_TILES
 PIECES_PER_CHUNK = CHUNK_TILES // PIECE_TILES
 
 X_BUFFERS = 6
-PRODUCT_LAG = 2
-PSUM_BANKS = 8
-ABREAST = 2
-SCALAR_BANKS = 3
-
-SORTED_PASSES = (3,)
-
-ROUND_MAGIC = 1.5 * 2.0**23
+PRODUCT_LAG = 1
 EXP_CAP = 2.0**60
+
+CFG = {"plan": {"0,4": "Q0","1,1": "VA0","1,4": "Q1","2,0": "M0 VEC","2,4": "Q2","3,0": "M1","3,2": "EX0 TH0","3,4": "Q3 CAP0","4,0": "M2","4,4": "Q4","5,0": "M3","5,2": "EX1 TH1","5,4": "CAP1 Q5 LN0 LN1","6,0": "M4","6,3": "ST0 ST1 U0 RN0","6,4": "Q6","7,0": "M5","7,1": "EX2 TH2","7,2": "U1","7,3": "CAP2","7,4": "Q7","8,0": "M6 WB0 M7 DC0 DC1 RN1 FR0 FR1 EX3 TH3 CAP3 LN2 LN3 DS0 DS1 BV0 BV1 ST2 ST3 U2 U3 RN2 RN3 FR2 FR3 SN0 AB0 CS0 SN1 AB1 CS1 RS0 RC0 RA0 RS1 RC1 RA1 SN2 AB2 CS2 SN3 AB3 CS3 RS2 RC2 RA2 RS3 RC3 BV2 BV3 DMP0 DMP1 RA3 DC2 DC3 DMP2 DMP3"},"sb": {"0": [0,1,2,3],"1": [1,2],"2": [0,2],"3": [0,2],"4": [0,2],"5": [0],"6": [0,1,2,3],"7": [0,2]},"wb": [],"xt": [0,1,2,3],"zdt": [4,6,7,4],"zph": [5,5,5,5],"rowb": {"B0": 6,"B1": 0,"S0": 1,"C0": 2,"S1": 3,"C1": 7,"S2": 5,"C2": 4,"S3": 1,"C3": 2,"D0": 3,"D1": 7,"D2": 5,"D3": 4,"B2": 6,"B3": 0},"sort": [3],"gdamp": [],"cap": "vector","wdt_cuts": [[0,1024],[1024,2048]],"x0_cuts": [[0,1024],[1024,2048]],"wb_after": 7,"vadd": [],"cb": [0,1,2,3]}
+PLAN = {tuple(int(v) for v in k.split(",")): v.split() for k, v in CFG["plan"].items()}
+SCALAR_BANKS = {int(k): tuple(v) for k, v in CFG["sb"].items()}
+W_BANKS = tuple(CFG["wb"])
+X_BUFFERS = 6
+WB_SLOT = 7
+BANKS = 8
+XT = tuple(CFG["xt"])
+ZDT = tuple(CFG["zdt"])
+ZPH = tuple(CFG["zph"])
+ROWB = CFG["rowb"]
+SORTED_PASSES = tuple(CFG["sort"])
+VEC_SLOT = 1
+CAP_ENGINE = CFG["cap"]
+G_DAMP = tuple(CFG['gdamp'])
 
 
 def tile_mamba3mimoblock_pa_kernel(
@@ -52,8 +62,21 @@ def tile_mamba3mimoblock_pa_kernel(
         stage = ctx.enter_context(tc.tile_pool(name="stage", bufs=3))
         keep = ctx.enter_context(tc.tile_pool(name="keep", bufs=1))
         chan = ctx.enter_context(tc.tile_pool(name="chan", bufs=CHUNKS))
+        chan3 = ctx.enter_context(tc.tile_pool(name="chan3", bufs=3))
         rows = ctx.enter_context(tc.tile_pool(name="rows", bufs=CHUNKS))
-        psum = ctx.enter_context(tc.psum_pool(name="psum", bufs=PSUM_BANKS))
+        rows3 = ctx.enter_context(tc.tile_pool(name="rows3", bufs=3))
+        rows2 = ctx.enter_context(tc.tile_pool(name="rows2", bufs=2))
+        psum = ctx.enter_context(tc.psum_pool(name="psum", bufs=8))
+        xt_count = [0]
+
+        def bank_tile(shape, which):
+            bank = psum.tile(shape, F32, name="bank", tag="bank")
+            return bank
+
+        def next_xt(shape):
+            xt_count[0] += 1
+            return bank_tile(shape, XT[(xt_count[0] - 1) % len(XT)])
+
         ctx.enter_context(tc.manual_schedule())
 
         x_rows = x.rearrange("(p t) k -> p t k", t=ROW_TILES)
@@ -66,46 +89,43 @@ def tile_mamba3mimoblock_pa_kernel(
             nc.scalar.dma_start(out=vec_rows[i : i + 1, :], in_=vec.rearrange("(o r) -> o r", o=1))
 
         w_sb = const.tile([P, 3, D], BF16)
-        nc.sync.dma_start(out=w_sb[:, 0, :], in_=W_dt)
+        for k0, k1 in CFG["wdt_cuts"]:
+            nc.sync.dma_start(out=w_sb[:, 0, k0:k1], in_=W_dt[:, k0:k1])
         nc.sync.dma_start(out=w_sb[:, 1, :], in_=W_ph)
         x_sb = []
         for piece in range(PIECES):
-            x_piece = xpool.tile([P, PIECE_TILES, D], BF16)
+            cuts = CFG["x0_cuts"] if piece == 0 else [[0, D]]
+            x_piece = xpool.tile([P, len(cuts), PIECE_TILES, D // len(cuts)], BF16, name="x_piece", tag="x_piece")
             t0 = piece * PIECE_TILES
-            nc.sync.dma_start(out=x_piece[:], in_=x_rows[:, t0 : t0 + PIECE_TILES, :])
+            for i, (k0, k1) in enumerate(cuts):
+                nc.sync.dma_start(out=x_piece[:, i], in_=x_rows[:, t0 : t0 + PIECE_TILES, k0:k1])
             x_sb.append(x_piece)
-        nc.sync.dma_start(out=w_sb[:, 2, :], in_=W_B)
-        st_re = const.tile([P, ROW_TILES, R], BF16)
-        st_im = const.tile([P, ROW_TILES, R], BF16)
-        nc.sync.dma_start(out=st_re[:], in_=state_re.rearrange("(p t) r -> p t r", t=ROW_TILES))
-        nc.sync.dma_start(out=st_im[:], in_=state_im.rearrange("(p t) r -> p t r", t=ROW_TILES))
+            if piece == CFG["wb_after"]:
+                nc.sync.dma_start(out=w_sb[:, 2, :], in_=W_B)
+        state = const.tile([P, 2, ROW_TILES, R], BF16)
+        nc.sync.dma_start(out=state[:, 0], in_=state_re.rearrange("(p t) r -> p t r", t=ROW_TILES))
+        nc.sync.dma_start(out=state[:, 1], in_=state_im.rearrange("(p t) r -> p t r", t=ROW_TILES))
 
         ident = const.tile([P, P], F32)
         make_identity(nc, ident[:])
 
-        def transposes_and_copies(words, n_tiles, scalar_banks, sorted_passes):
+        def transposes_and_copies(words, n_tiles, scalar_banks, presorted=None, slot=None):
             grouped = stage.tile([P, PASSES * n_tiles * P * PACK], BF16, tag="grouped", align_bytes=64)
             grouped_words = grouped[:].bitcast(F32).rearrange("q (g c u) -> q g c u", g=PASSES, u=2)
             for g in range(PASSES):
-                bank = psum.tile([P, 2, n_tiles, P], F32, tag="bank")
-                pass_words = words[:, :, g * WORDS_PASS : (g + 1) * WORDS_PASS]
-                if g in sorted_passes:
-                    by_parity = stage.tile([P, n_tiles, 2, P], F32, tag="by_parity")
-                    nc.gpsimd.tensor_copy(
-                        out=by_parity[:], in_=pass_words.rearrange("p j (q u) -> p j u q", u=2)
-                    )
+                bank = next_xt([P, 2, n_tiles, P])
+                pass_words = pass_of(slot, g) if slot is not None else words[:, :, g * WORDS_PASS : (g + 1) * WORDS_PASS]
                 for u in range(2):
                     for j in range(n_tiles):
-                        if g in sorted_passes:
-                            chosen = by_parity[:, j, u, :]
-                        else:
-                            chosen = pass_words[:, j, u:WORDS_PASS:2]
+                        chosen = presorted[g][:, j, u, :] if presorted and g in presorted else pass_words[:, j, u:WORDS_PASS:2]
                         nc.tensor.transpose(bank[:, u, j, :], chosen, ident[:])
                 halves = bank[:].rearrange("q u j p -> q (j p) u")
-                if g < scalar_banks:
+                if g in scalar_banks:
                     nc.scalar.copy(out=grouped_words[:, g], in_=halves)
                 else:
                     nc.vector.tensor_copy(out=grouped_words[:, g], in_=halves)
+                if slot is not None:
+                    follow(slot, g)
             return grouped
 
         w_words = w_sb[:].bitcast(F32)
@@ -113,40 +133,53 @@ def tile_mamba3mimoblock_pa_kernel(
         w2_scales = keep.tile([P, PASSES, 2, P], U8, align_bytes=64)
         wb_codes = keep.tile([P, PASSES, P], U32, align_bytes=64)
         wb_scales = keep.tile([P, PASSES, P], U8, align_bytes=64)
-        w2_grouped = transposes_and_copies(w_words[:, 0:2, :], 2, 2, ())
+        w2_grouped = transposes_and_copies(w_words[:, 0:2, :], 2, W_BANKS)
         nc.vector.quantize_mx(
             out=w2_codes[:].rearrange("q g j r -> q (g j r)").bitcast(FP8X4),
             scales=w2_scales[:].rearrange("q g j r -> q (g j r)"),
             in_=w2_grouped[:],
         )
 
-        vec_f32 = const.tile([P, P], F32)
-        nc.vector.tensor_copy(out=vec_f32[:], in_=vec_rows[:])
-        vec_t = psum.tile([P, P], F32, tag="bank")
-        nc.tensor.transpose(vec_t[:], vec_f32[:], ident[:])
-        per_chan = const.tile([P, 4], F32)
-        nc.vector.tensor_copy(out=per_chan[:], in_=vec_t[:, 0:4])
-        b_dt_col = per_chan[:, 0:1]
-        b_ph_col = per_chan[:, 1:2]
-        a_col = const.tile([P, 1], F32)
-        nc.scalar.activation(out=a_col[:], in_=per_chan[:, 2:3], func=ACT.Exp)
-        neg_a_col = const.tile([P, 1], F32)
-        nc.vector.tensor_scalar_mul(out=neg_a_col[:], in0=a_col[:], scalar1=-1.0)
-        turns_col = const.tile([P, 1], F32)
-        nc.vector.tensor_scalar_mul(out=turns_col[:], in0=per_chan[:, 3:4], scalar1=1.0 / (2.0 * math.pi))
+        cols = {}
+
+        def vec_copy(c):
+            cols["vec"] = const.tile([P, P], F32, name="vec_f32")
+            nc.vector.tensor_copy(out=cols["vec"][:], in_=vec_rows[:])
+
+        def channel_constants():
+            vec_f32 = cols["vec"]
+            vec_t = bank_tile([P, P], 7)
+            nc.tensor.transpose(vec_t[:], vec_f32[:], ident[:])
+            per_chan = const.tile([P, 4], F32, name="per_chan")
+            nc.vector.tensor_copy(out=per_chan[:], in_=vec_t[:, 0:4])
+            cols["b_dt"] = per_chan[:, 0:1]
+            cols["b_ph"] = per_chan[:, 1:2]
+            a_col = const.tile([P, 1], F32, name="a_col")
+            nc.scalar.activation(out=a_col[:], in_=per_chan[:, 2:3], func=ACT.Exp)
+            neg_a_col = const.tile([P, 1], F32, name="neg_a_col")
+            nc.gpsimd.tensor_scalar(out=neg_a_col[:], in0=a_col[:], scalar1=-1.0, scalar2=0.0, op0=ALU.mult, op1=ALU.add)
+            cols["neg_a"] = neg_a_col[:]
+            half_turns_col = const.tile([P, 1], F32, name="half_turns_col")
+            nc.vector.tensor_scalar_mul(out=half_turns_col[:], in0=per_chan[:, 3:4], scalar1=1.0 / math.pi)
+            cols["half_turns"] = half_turns_col[:]
 
         x_codes = keep.tile([P, PIECES, PASSES, PIECE_TILES, P], U32, align_bytes=64)
         x_scales = keep.tile([P, PIECES, PASSES, PIECE_TILES, P], U8, align_bytes=64)
-        z_dt = {}
-        z_ph = {}
-        z_b = {}
-        soft = {}
-        turn = {}
-        frac = {}
-        sine = {}
-        cosine = {}
-        re_part = {}
-        im_part = {}
+        turns, z_dt, z_ph, z_b, soft, turn, frac, sine, cosine, parts = {}, {}, {}, {}, {}, {}, {}, {}, {}, {}
+
+        def pass_of(piece, g):
+            words = x_sb[piece][:].bitcast(F32)
+            per_cut = PASSES // words.shape[1]
+            return words[:, g // per_cut, :, (g % per_cut) * WORDS_PASS : (g % per_cut + 1) * WORDS_PASS]
+
+        def sort_words(piece):
+            out = {}
+            for g in (CFG['sortp'][piece] if 'sortp' in CFG else SORTED_PASSES):
+                by_parity = stage.tile([P, PIECE_TILES, 2, P], F32, name="by_parity", tag="by_parity", bufs=6)
+                pass_words = pass_of(piece, g)
+                nc.gpsimd.tensor_copy(out=by_parity[:], in_=pass_words.rearrange("p j (q u) -> p j u q", u=2))
+                out[g] = by_parity
+            return out
 
         def quantise(piece, grouped):
             nc.vector.quantize_mx(
@@ -159,8 +192,8 @@ def tile_mamba3mimoblock_pa_kernel(
             c = piece // PIECES_PER_CHUNK
             half = piece % PIECES_PER_CHUNK
             if half == 0:
-                z_dt[c] = psum.tile([P, CHUNK_COLS], F32, name="z_dt", tag="bank")
-                z_ph[c] = psum.tile([P, CHUNK_COLS], F32, name="z_ph", tag="bank")
+                z_dt[c] = bank_tile([P, CHUNK_COLS], ZDT[c])
+                z_ph[c] = bank_tile([P, CHUNK_COLS], ZPH[c])
             cols = slice(half * PIECE_COLS, (half + 1) * PIECE_COLS)
             for i, z in enumerate((z_dt[c], z_ph[c])):
                 for g in range(PASSES):
@@ -174,16 +207,26 @@ def tile_mamba3mimoblock_pa_kernel(
                         stop=(g == PASSES - 1),
                     )
 
-        def exp_and_tanh(c):
+        def exp_of(c):
             soft[c] = chan.tile([P, CHUNK_COLS], F32, name="soft", tag="soft")
+            nc.scalar.activation(out=soft[c][:], in_=z_dt[c][:], func=ACT.Exp, bias=cols["b_dt"], scale=1.0)
+
+        def tanh_of(c):
             turn[c] = chan.tile([P, CHUNK_COLS], F32, name="turn", tag="turn")
-            nc.scalar.activation(out=soft[c][:], in_=z_dt[c][:], func=ACT.Exp, bias=b_dt_col, scale=1.0)
-            nc.scalar.activation(out=turn[c][:], in_=z_ph[c][:], func=ACT.Tanh, bias=b_ph_col, scale=1.0)
-            nc.vector.tensor_scalar_min(out=soft[c][:], in0=soft[c][:], scalar1=EXP_CAP)
-            nc.vector.tensor_scalar_mul(out=turn[c][:], in0=turn[c][:], scalar1=0.5)
+            nc.scalar.activation(out=turn[c][:], in_=z_ph[c][:], func=ACT.Tanh, bias=cols["b_ph"], scale=1.0)
+
+        def cap(c):
+            if CAP_ENGINE == "gpsimd":
+                nc.gpsimd.tensor_scalar(
+                    out=soft[c][:], in0=soft[c][:], scalar1=EXP_CAP, scalar2=1.0, op0=ALU.min, op1=ALU.add
+                )
+            else:
+                nc.vector.tensor_scalar(
+                    out=soft[c][:], in0=soft[c][:], scalar1=EXP_CAP, scalar2=1.0, op0=ALU.min, op1=ALU.add
+                )
 
         def b_val(c):
-            z_b[c] = psum.tile([P, CHUNK_TILES, R], F32, name="z_b", tag="bank")
+            z_b[c] = bank_tile([P, CHUNK_TILES, R], ROWB["B%d" % c])
             for jj in range(CHUNK_TILES):
                 piece = (c * CHUNK_TILES + jj) // PIECE_TILES
                 j = (c * CHUNK_TILES + jj) % PIECE_TILES
@@ -199,129 +242,126 @@ def tile_mamba3mimoblock_pa_kernel(
                     )
 
         def logarithm(c):
-            nc.scalar.activation(out=soft[c][:], in_=soft[c][:], func=ACT.Ln, bias=1.0, scale=1.0)
+            nc.scalar.activation(out=soft[c][:], in_=soft[c][:], func=ACT.Ln)
 
         def step_size(c):
             nc.vector.scalar_tensor_tensor(
-                out=soft[c][:], in0=z_dt[c][:], scalar=b_dt_col, in1=soft[c][:], op0=ALU.add, op1=ALU.max
+                out=soft[c][:], in0=z_dt[c][:], scalar=cols["b_dt"], in1=soft[c][:], op0=ALU.add, op1=ALU.max
             )
 
-        def angle_in_turns(c):
+        def angle(c):
             nc.vector.scalar_tensor_tensor(
-                out=turn[c][:], in0=soft[c][:], scalar=turns_col[:], in1=turn[c][:], op0=ALU.mult, op1=ALU.add
+                out=turn[c][:], in0=soft[c][:], scalar=cols["half_turns"], in1=turn[c][:], op0=ALU.mult, op1=ALU.add
             )
 
-        def nearest_turn(c):
-            frac[c] = chan.tile([P, CHUNK_COLS], F32, name="frac", tag="frac")
-            nc.vector.tensor_scalar(
-                out=frac[c][:], in0=turn[c][:], scalar1=ROUND_MAGIC, scalar2=ROUND_MAGIC,
-                op0=ALU.add, op1=ALU.subtract,
-            )
+        def nearest_even(c):
+            turns[c] = chan3.tile([P, CHUNK_COLS], I32, name="turns", tag="turns")
+            nc.vector.tensor_scalar_mul(out=turns[c][:], in0=turn[c][:], scalar1=0.5)
 
         def fraction(c):
-            nc.vector.tensor_sub(out=frac[c][:], in0=frac[c][:], in1=turn[c][:])
+            frac[c] = turn[c]
+            nc.vector.scalar_tensor_tensor(
+                out=frac[c][:], in0=turns[c][:], scalar=2.0, in1=turn[c][:], op0=ALU.mult, op1=ALU.subtract
+            )
 
         def sine_of(c):
-            sine[c] = chan.tile([P, CHUNK_COLS], F32, name="sine", tag="sine")
-            nc.scalar.activation(out=sine[c][:], in_=frac[c][:], func=ACT.Sin, scale=-2.0 * math.pi)
+            sine[c] = chan3.tile([P, CHUNK_COLS], F32, name="sine", tag="sine")
+            nc.scalar.activation(out=sine[c][:], in_=frac[c][:], func=ACT.Sin, scale=-math.pi)
 
         def magnitude_of(c):
-            cosine[c] = chan.tile([P, CHUNK_COLS], F32, name="cosine", tag="cosine")
+            cosine[c] = chan3.tile([P, CHUNK_COLS], F32, name="cosine", tag="cosine")
             nc.scalar.activation(out=cosine[c][:], in_=frac[c][:], func=ACT.Abs)
 
         def cosine_of(c):
             nc.scalar.activation(
-                out=cosine[c][:], in_=cosine[c][:], func=ACT.Sin, scale=-2.0 * math.pi, bias=math.pi / 2.0
+                out=cosine[c][:], in_=cosine[c][:], func=ACT.Sin, scale=-math.pi, bias=math.pi / 2.0
             )
 
         def decay(c):
-            nc.scalar.activation(out=soft[c][:], in_=soft[c][:], func=ACT.Exp, scale=neg_a_col[:])
+            nc.scalar.activation(out=soft[c][:], in_=soft[c][:], func=ACT.Exp, scale=cols["neg_a"])
 
-        def back_to_rows(channel_tile):
-            bank = psum.tile([P, CHUNK_TILES, R], F32, name="row_bank", tag="bank")
+        def back_to_rows(channel_tile, which):
+            bank = bank_tile([P, CHUNK_TILES, R], ROWB[which])
             for jj in range(CHUNK_TILES):
                 nc.tensor.transpose(bank[:, jj, :], channel_tile[:, jj * P : (jj + 1) * P], ident[:])
             return bank
 
-        def rotate(c):
+        def both(bank):
+            return bank[:].rearrange("p t r -> p (t r)").unsqueeze(1).broadcast_to([P, 2, CHUNK_COLS])
+
+        by_sin, by_cos, damped = {}, {}, {}
+
+        def damp_state(c):
             t0 = c * CHUNK_TILES
-            sr = st_re[:, t0 : t0 + CHUNK_TILES, :]
-            si = st_im[:, t0 : t0 + CHUNK_TILES, :]
-            sin_t = back_to_rows(sine[c])
-            cos_t = back_to_rows(cosine[c])
-            re_sin = rows.tile([P, CHUNK_TILES, R], F32, tag="re_sin")
-            im_sin = rows.tile([P, CHUNK_TILES, R], F32, tag="im_sin")
-            re_cos = rows.tile([P, CHUNK_TILES, R], F32, tag="re_cos")
-            im_cos = rows.tile([P, CHUNK_TILES, R], F32, tag="im_cos")
-            nc.vector.tensor_mul(out=re_sin[:], in0=sr, in1=sin_t[:])
-            nc.vector.tensor_mul(out=im_sin[:], in0=si, in1=sin_t[:])
-            nc.vector.tensor_mul(out=re_cos[:], in0=sr, in1=cos_t[:])
-            nc.vector.tensor_mul(out=im_cos[:], in0=si, in1=cos_t[:])
-            nc.gpsimd.tensor_add(out=re_sin[:], in0=re_sin[:], in1=im_cos[:])
-            nc.gpsimd.tensor_sub(out=re_cos[:], in0=re_cos[:], in1=im_sin[:])
-            im_part[c] = re_sin
-            re_part[c] = re_cos
+            st = state[:, :, t0 : t0 + CHUNK_TILES, :].rearrange("p c t r -> p c (t r)")
+            damped[c] = rows2.tile([P, 2, CHUNK_COLS], F32, name="damped", tag="damped")
+            nc.vector.tensor_mul(out=damped[c][:], in0=st, in1=both(back_to_rows(soft[c], "D%d" % c)))
+
+        def rot_sin(c):
+            t0 = c * CHUNK_TILES
+            st = damped[c][:] if c in damped else state[:, :, t0 : t0 + CHUNK_TILES, :].rearrange("p c t r -> p c (t r)")
+            by_sin[c] = rows3.tile([P, 2, CHUNK_COLS], F32, name="by_sin", tag="by_sin")
+            nc.vector.tensor_mul(out=by_sin[c][:], in0=st, in1=both(back_to_rows(sine[c], "S%d" % c)))
+
+        def rot_cos(c):
+            t0 = c * CHUNK_TILES
+            st = damped[c][:] if c in damped else state[:, :, t0 : t0 + CHUNK_TILES, :].rearrange("p c t r -> p c (t r)")
+            by_cos[c] = rows.tile([P, 2, CHUNK_COLS], F32, name="by_cos", tag="by_cos")
+            nc.vector.tensor_mul(out=by_cos[c][:], in0=st, in1=both(back_to_rows(cosine[c], "C%d" % c)))
+
+        def rot_add(c):
+            parts[c] = by_cos[c]
+            eng = nc.vector if c in CFG["vadd"] else nc.gpsimd
+            eng.tensor_sub(out=parts[c][:, 0], in0=by_cos[c][:, 0], in1=by_sin[c][:, 1])
+            eng.tensor_add(out=parts[c][:, 1], in0=by_cos[c][:, 1], in1=by_sin[c][:, 0])
 
         def damp_and_store(c):
             t0 = c * CHUNK_TILES
-            decay_t = back_to_rows(soft[c])
-            nc.vector.tensor_mul(out=re_part[c][:], in0=re_part[c][:], in1=decay_t[:])
-            nc.vector.tensor_mul(out=im_part[c][:], in0=im_part[c][:], in1=decay_t[:])
-            nc.sync.dma_start(out=im_rows[:, t0 : t0 + CHUNK_TILES, :], in_=im_part[c][:])
-            nc.vector.tensor_add(out=re_part[c][:], in0=re_part[c][:], in1=z_b[c][:])
-            nc.sync.dma_start(out=re_rows[:, t0 : t0 + CHUNK_TILES, :], in_=re_part[c][:])
+            decay_t = None if c in damped else back_to_rows(soft[c], "D%d" % c)
+            if c in damped:
+                pass
+            elif c in G_DAMP:
+                decay_rows = rows.tile([P, CHUNK_COLS], F32, name="decay_rows", tag="decay_rows")
+                nc.scalar.copy(out=decay_rows[:], in_=decay_t[:].rearrange("p t r -> p (t r)"))
+                for i in range(2):
+                    nc.gpsimd.tensor_mul(out=parts[c][:, i], in0=parts[c][:, i], in1=decay_rows[:])
+            else:
+                nc.vector.tensor_mul(out=parts[c][:], in0=parts[c][:], in1=both(decay_t))
+            nc.sync.dma_start(out=im_rows[:, t0 : t0 + CHUNK_TILES, :], in_=parts[c][:, 1].rearrange("p (t r) -> p t r", r=R))
+            nc.vector.tensor_add(out=parts[c][:, 0], in0=parts[c][:, 0], in1=z_b[c][:].rearrange("p t r -> p (t r)"))
+            nc.sync.dma_start(out=re_rows[:, t0 : t0 + CHUNK_TILES, :], in_=parts[c][:, 0].rearrange("p (t r) -> p t r", r=R))
 
-        def angles(abreast):
-            for c in abreast:
-                step_size(c)
-            for c in abreast:
-                angle_in_turns(c)
-            for c in abreast:
-                nearest_turn(c)
-            for c in abreast:
-                fraction(c)
+        steps = {
+            "EX": exp_of, "TH": tanh_of, "CAP": cap, "LN": logarithm, "ST": step_size, "U": angle, "RN": nearest_even,
+            "FR": fraction, "SN": sine_of, "AB": magnitude_of, "CS": cosine_of, "DC": decay, "BV": b_val, "RS": rot_sin, "RC": rot_cos, "RA": rot_add, "DS": damp_state,
+            "DMP": damp_and_store,
+        }
 
-        first_half = range(0, CHUNKS // 2)
-        second_half = range(CHUNKS // 2, CHUNKS)
+        sorted_words, grouped = {}, {}
+        steps["M"] = products
+        steps["Q"] = lambda c: quantise(c, grouped[c])
+        def weights_b(c):
+            wb_grouped = transposes_and_copies(w_words[:, 2:3, :], 1, tuple(CFG.get("cb", (0, 2))))
+            nc.vector.quantize_mx(
+                out=wb_codes[:].rearrange("q g r -> q (g r)").bitcast(FP8X4),
+                scales=wb_scales[:].rearrange("q g r -> q (g r)"),
+                in_=wb_grouped[:],
+            )
+        steps["WB"] = weights_b
 
+        def follow(slot, g):
+            for step in PLAN.get((slot, g), []):
+                if step == "VA0":
+                    vec_copy(0)
+                elif step == "VEC":
+                    channel_constants()
+                else:
+                    steps[step[:-1]](int(step[-1:]))
+
+        sorted_words[0] = sort_words(0)
         for piece in range(PIECES):
-            quantise(piece, transposes_and_copies(x_sb[piece][:].bitcast(F32), PIECE_TILES, SCALAR_BANKS, SORTED_PASSES))
-            behind = piece - PRODUCT_LAG
-            if 0 <= behind < PIECES // 2:
-                products(behind)
-                if behind % PIECES_PER_CHUNK == PIECES_PER_CHUNK - 1:
-                    exp_and_tanh(behind // PIECES_PER_CHUNK)
-
-        for c in first_half:
-            logarithm(c)
-        wb_grouped = transposes_and_copies(w_words[:, 2:3, :], 1, 0, ())
-        nc.vector.quantize_mx(
-            out=wb_codes[:].rearrange("q g r -> q (g r)").bitcast(FP8X4),
-            scales=wb_scales[:].rearrange("q g r -> q (g r)"),
-            in_=wb_grouped[:],
-        )
-        for piece in range(PIECES // 2, PIECES):
-            products(piece)
-        angles(first_half)
-        for c in second_half:
-            exp_and_tanh(c)
-        for c in range(CHUNKS):
-            b_val(c)
-        for c in second_half:
-            logarithm(c)
-        angles(second_half)
-
-        for first in range(0, CHUNKS, ABREAST):
-            abreast = range(first, first + ABREAST)
-            for c in abreast:
-                sine_of(c)
-            for c in abreast:
-                magnitude_of(c)
-            for c in abreast:
-                cosine_of(c)
-        for c in range(CHUNKS):
-            decay(c)
-        for c in range(CHUNKS):
-            rotate(c)
-        for c in range(CHUNKS):
-            damp_and_store(c)
+            if piece + 1 < PIECES:
+                sorted_words[piece + 1] = sort_words(piece + 1)
+            grouped[piece] = (transposes_and_copies(None, PIECE_TILES, SCALAR_BANKS[piece], sorted_words[piece], piece))
+            follow(piece, 4)
+        follow(PIECES, 0)

@@ -35,7 +35,7 @@ X_BUFFERS = 6
 PRODUCT_LAG = 1
 EXP_CAP = 2.0**60
 
-CFG = {"plan": {"0,4": "Q0","1,1": "VA0","1,4": "Q1","2,0": "M0 VEC","2,4": "Q2","3,0": "M1","3,2": "EX0 TH0","3,4": "Q3 CAP0","4,0": "M2","4,4": "Q4","5,0": "M3","5,2": "EX1 TH1","5,4": "CAP1 Q5 LN0 LN1","6,0": "M4","6,3": "ST0 ST1 U0 RN0","6,4": "Q6","7,0": "M5","7,1": "EX2 TH2","7,2": "U1","7,3": "CAP2","7,4": "Q7","8,0": "M6 WB0 M7 DC0 DC1 RN1 FR0 FR1 EX3 TH3 CAP3 LN2 LN3 DS0 DS1 BV0 BV1 ST2 ST3 U2 U3 RN2 RN3 FR2 FR3 SN0 AB0 CS0 SN1 AB1 CS1 RS0 RC0 RA0 RS1 RC1 RA1 SN2 AB2 CS2 SN3 AB3 CS3 RS2 RC2 RA2 RS3 RC3 BV2 BV3 DMP0 DMP1 RA3 DC2 DC3 DMP2 DMP3"},"sb": {"0": [0,1,2,3],"1": [1,2],"2": [0,2],"3": [0,2],"4": [0,2],"5": [0],"6": [0,1,2,3],"7": [0,2]},"wb": [],"xt": [0,1,2,3],"zdt": [4,6,7,4],"zph": [5,5,5,5],"rowb": {"B0": 6,"B1": 0,"S0": 1,"C0": 2,"S1": 3,"C1": 7,"S2": 5,"C2": 4,"S3": 1,"C3": 2,"D0": 3,"D1": 7,"D2": 5,"D3": 4,"B2": 6,"B3": 0},"sort": [3],"gdamp": [],"cap": "vector","wdt_cuts": [[0,1024],[1024,2048]],"x0_cuts": [[0,1024],[1024,2048]],"wb_after": 7,"vadd": [],"cb": [0,1,2,3]}
+CFG = {"plan": {"0,4": "Q0","1,1": "VA0","1,4": "Q1 M0","2,0": "","2,4": "Q2","3,0": "M1","3,2": "EX0 TH0","3,4": "Q3 CAP0","4,0": "M2","4,4": "Q4","5,0": "M3","5,2": "EX1 TH1","5,4": "CAP1 Q5 LN0 LN1","6,0": "M4","6,3": "ST0 ST1 U0 RN0","6,4": "Q6","7,0": "M5","7,1": "EX2 TH2","7,2": "U1","7,3": "CAP2","7,4": "Q7","8,0": "M6 WB0 M7 DC0 DC1 RN1 FR0 FR1 EX3 TH3 CAP3 LN2 LN3 DS0 DS1 BV0 BV1 ST2 ST3 U2 U3 RN2 RN3 FR2 FR3 SN0 AB0 CS0 SN1 AB1 CS1 RS0 RC0 RA0 RS1 RC1 RA1 SN2 AB2 CS2 SN3 AB3 CS3 RS2 RC2 RA2 RS3 RC3 BV2 BV3 DMP0 DMP1 RA3 DC2 DC3 DMP2 DMP3","2,1": "VEC VS3","1,3": "VS2","3,1": "VS4","4,1": "VS5"},"sb": {"0": [1,3],"1": [1,2],"2": [0,2],"3": [0,2],"4": [0,2],"5": [0],"6": [0,1,2,3],"7": [0,2]},"wb": [[],[0,2]],"xt": [0,1,2,3],"zdt": [4,6,7,4],"zph": [5,5,5,5],"rowb": {"B0": 6,"B1": 0,"S0": 1,"C0": 2,"S1": 3,"C1": 7,"S2": 5,"C2": 4,"S3": 1,"C3": 2,"D0": 3,"D1": 7,"D2": 5,"D3": 4,"B2": 6,"B3": 0},"sort": [3],"gdamp": [],"cap": "vector","wdt_cuts": [[0,1024],[1024,2048]],"x0_cuts": [[0,1024],[1024,2048]],"wb_after": 7,"vadd": [],"cb": [0,1,2,3],"first_w": [0,1],"loads": [["w",0,0,2],["w",0,1,2],["w",1,0,1],["x",0,0,2],["x",0,1,2],["x",1,0,2],["x",1,1,2],["x",2,0,1],["x",3,0,1],["x",4,0,1],["x",5,0,1],["x",6,0,1],["x",7,0,1],["w",2,0,1]],"sortp": [[],[],[3],[3],[3],[3],[3],[3]],"vs": {"2": [[2,"s"]],"3": [[2,"s"]],"4": [[2,"s"]],"5": [[2,"s"]]}}
 PLAN = {tuple(int(v) for v in k.split(",")): v.split() for k, v in CFG["plan"].items()}
 SCALAR_BANKS = {int(k): tuple(v) for k, v in CFG["sb"].items()}
 W_BANKS = tuple(CFG["wb"])
@@ -89,19 +89,24 @@ def tile_mamba3mimoblock_pa_kernel(
             nc.scalar.dma_start(out=vec_rows[i : i + 1, :], in_=vec.rearrange("(o r) -> o r", o=1))
 
         w_sb = const.tile([P, 3, D], BF16)
-        for k0, k1 in CFG["wdt_cuts"]:
-            nc.sync.dma_start(out=w_sb[:, 0, k0:k1], in_=W_dt[:, k0:k1])
-        nc.sync.dma_start(out=w_sb[:, 1, :], in_=W_ph)
-        x_sb = []
-        for piece in range(PIECES):
-            cuts = CFG["x0_cuts"] if piece == 0 else [[0, D]]
-            x_piece = xpool.tile([P, len(cuts), PIECE_TILES, D // len(cuts)], BF16, name="x_piece", tag="x_piece")
+        x_sb = {}
+
+        def load_weight(i, part, parts_of):
+            k0, k1 = part * D // parts_of, (part + 1) * D // parts_of
+            nc.sync.dma_start(out=w_sb[:, i, k0:k1], in_=(W_dt, W_ph, W_B)[i][:, k0:k1])
+
+        def load_x(piece, part, parts_of):
+            if part == 0:
+                x_sb[piece] = xpool.tile([P, parts_of, PIECE_TILES, D // parts_of], BF16, name="x_piece", tag="x_piece")
+            k0, k1 = part * D // parts_of, (part + 1) * D // parts_of
             t0 = piece * PIECE_TILES
-            for i, (k0, k1) in enumerate(cuts):
-                nc.sync.dma_start(out=x_piece[:, i], in_=x_rows[:, t0 : t0 + PIECE_TILES, k0:k1])
-            x_sb.append(x_piece)
-            if piece == CFG["wb_after"]:
-                nc.sync.dma_start(out=w_sb[:, 2, :], in_=W_B)
+            nc.sync.dma_start(out=x_sb[piece][:, part], in_=x_rows[:, t0 : t0 + PIECE_TILES, k0:k1])
+
+        for kind, i, part, parts_of in CFG["loads"]:
+            if kind == "w":
+                load_weight(i, part, parts_of)
+            else:
+                load_x(i, part, parts_of)
         state = const.tile([P, 2, ROW_TILES, R], BF16)
         nc.sync.dma_start(out=state[:, 0], in_=state_re.rearrange("(p t) r -> p t r", t=ROW_TILES))
         nc.sync.dma_start(out=state[:, 1], in_=state_im.rearrange("(p t) r -> p t r", t=ROW_TILES))
@@ -110,8 +115,10 @@ def tile_mamba3mimoblock_pa_kernel(
         make_identity(nc, ident[:])
 
         def transposes_and_copies(words, n_tiles, scalar_banks, presorted=None, slot=None):
-            grouped = stage.tile([P, PASSES * n_tiles * P * PACK], BF16, tag="grouped", align_bytes=64)
-            grouped_words = grouped[:].bitcast(F32).rearrange("q (g c u) -> q g c u", g=PASSES, u=2)
+            out_tile = stage.tile([P, PASSES * n_tiles * P * PACK], BF16, name="grouped", tag="grouped", align_bytes=64)
+            if slot is not None:
+                grouped[slot] = out_tile
+            grouped_words = out_tile[:].bitcast(F32).rearrange("q (g c u) -> q g c u", g=PASSES, u=2)
             for g in range(PASSES):
                 bank = next_xt([P, 2, n_tiles, P])
                 pass_words = pass_of(slot, g) if slot is not None else words[:, :, g * WORDS_PASS : (g + 1) * WORDS_PASS]
@@ -126,19 +133,20 @@ def tile_mamba3mimoblock_pa_kernel(
                     nc.vector.tensor_copy(out=grouped_words[:, g], in_=halves)
                 if slot is not None:
                     follow(slot, g)
-            return grouped
+            return out_tile
 
         w_words = w_sb[:].bitcast(F32)
-        w2_codes = keep.tile([P, PASSES, 2, P], U32, align_bytes=64)
-        w2_scales = keep.tile([P, PASSES, 2, P], U8, align_bytes=64)
+        w2_codes = keep.tile([P, 2, PASSES, P], U32, align_bytes=64)
+        w2_scales = keep.tile([P, 2, PASSES, P], U8, align_bytes=64)
         wb_codes = keep.tile([P, PASSES, P], U32, align_bytes=64)
         wb_scales = keep.tile([P, PASSES, P], U8, align_bytes=64)
-        w2_grouped = transposes_and_copies(w_words[:, 0:2, :], 2, W_BANKS)
-        nc.vector.quantize_mx(
-            out=w2_codes[:].rearrange("q g j r -> q (g j r)").bitcast(FP8X4),
-            scales=w2_scales[:].rearrange("q g j r -> q (g j r)"),
-            in_=w2_grouped[:],
-        )
+        def weights_a(i):
+            w2_grouped = transposes_and_copies(w_words[:, i : i + 1, :], 1, W_BANKS[i])
+            nc.vector.quantize_mx(
+                out=w2_codes[:, i].rearrange("q g r -> q (g r)").bitcast(FP8X4),
+                scales=w2_scales[:, i].rearrange("q g r -> q (g r)"),
+                in_=w2_grouped[:],
+            )
 
         cols = {}
 
@@ -162,7 +170,9 @@ def tile_mamba3mimoblock_pa_kernel(
             half_turns_col = const.tile([P, 1], F32, name="half_turns_col")
             nc.vector.tensor_scalar_mul(out=half_turns_col[:], in0=per_chan[:, 3:4], scalar1=1.0 / math.pi)
             cols["half_turns"] = half_turns_col[:]
+            cols["scratch"] = const.tile([P, 1], F32, name="scratch")[:]
 
+        grouped = {}
         x_codes = keep.tile([P, PIECES, PASSES, PIECE_TILES, P], U32, align_bytes=64)
         x_scales = keep.tile([P, PIECES, PASSES, PIECE_TILES, P], U8, align_bytes=64)
         turns, z_dt, z_ph, z_b, soft, turn, frac, sine, cosine, parts = {}, {}, {}, {}, {}, {}, {}, {}, {}, {}
@@ -181,11 +191,30 @@ def tile_mamba3mimoblock_pa_kernel(
                 out[g] = by_parity
             return out
 
+        def vector_sort(piece):
+            for g, eng in CFG["vs"][str(piece)]:
+                by_parity = stage.tile([P, PIECE_TILES, 2, P], F32, name="by_parity", tag="by_parity", bufs=6)
+                src = pass_of(piece, g).rearrange("p j (q u) -> p j u q", u=2)
+                if eng == "v":
+                    nc.vector.tensor_copy(out=by_parity[:], in_=src)
+                else:
+                    nc.scalar.copy(out=by_parity[:], in_=src)
+                sorted_words.setdefault(piece, {})[g] = by_parity
+
         def quantise(piece, grouped):
             nc.vector.quantize_mx(
                 out=x_codes[:, piece].rearrange("q g j p -> q (g j p)").bitcast(FP8X4),
                 scales=x_scales[:, piece].rearrange("q g j p -> q (g j p)"),
                 in_=grouped[:],
+            )
+
+        def quantise_half(piece, half):
+            cut = PASSES // 2
+            width = PASSES * PIECE_TILES * P * PACK // 2
+            nc.vector.quantize_mx(
+                out=x_codes[:, piece, half * cut : (half + 1) * cut].rearrange("q g j p -> q (g j p)").bitcast(FP8X4),
+                scales=x_scales[:, piece, half * cut : (half + 1) * cut].rearrange("q g j p -> q (g j p)"),
+                in_=grouped[piece][:, half * width : (half + 1) * width],
             )
 
         def products(piece):
@@ -199,8 +228,8 @@ def tile_mamba3mimoblock_pa_kernel(
                 for g in range(PASSES):
                     nc.tensor.matmul_mx(
                         out=z[:, cols],
-                        lhsT=w2_codes[:, g, i, :].bitcast(FP8X4),
-                        lhsT_scale=w2_scales[:, g, i, :],
+                        lhsT=w2_codes[:, i, g, :].bitcast(FP8X4),
+                        lhsT_scale=w2_scales[:, i, g, :],
                         rhs=x_codes[:, piece, g].rearrange("q j p -> q (j p)").bitcast(FP8X4),
                         rhs_scale=x_scales[:, piece, g].rearrange("q j p -> q (j p)"),
                         start=(g == 0),
@@ -263,6 +292,9 @@ def tile_mamba3mimoblock_pa_kernel(
             nc.vector.scalar_tensor_tensor(
                 out=frac[c][:], in0=turns[c][:], scalar=2.0, in1=turn[c][:], op0=ALU.mult, op1=ALU.subtract
             )
+
+        def silu_table(c):
+            nc.scalar.activation(out=cols["scratch"], in_=cols["b_dt"], func=ACT.Silu)
 
         def sine_of(c):
             sine[c] = chan3.tile([P, CHUNK_COLS], F32, name="sine", tag="sine")
@@ -333,12 +365,15 @@ def tile_mamba3mimoblock_pa_kernel(
 
         steps = {
             "EX": exp_of, "TH": tanh_of, "CAP": cap, "LN": logarithm, "ST": step_size, "U": angle, "RN": nearest_even,
-            "FR": fraction, "SN": sine_of, "AB": magnitude_of, "CS": cosine_of, "DC": decay, "BV": b_val, "RS": rot_sin, "RC": rot_cos, "RA": rot_add, "DS": damp_state,
+            "FR": fraction, "SN": sine_of, "TT": silu_table, "AB": magnitude_of, "CS": cosine_of, "DC": decay, "BV": b_val, "RS": rot_sin, "RC": rot_cos, "RA": rot_add, "DS": damp_state,
             "DMP": damp_and_store,
         }
 
-        sorted_words, grouped = {}, {}
+        sorted_words = {}
         steps["M"] = products
+        steps["VS"] = vector_sort
+        steps["QA"] = lambda c: quantise_half(c, 0)
+        steps["QZ"] = lambda c: quantise_half(c, 1)
         steps["Q"] = lambda c: quantise(c, grouped[c])
         def weights_b(c):
             wb_grouped = transposes_and_copies(w_words[:, 2:3, :], 1, tuple(CFG.get("cb", (0, 2))))
@@ -348,6 +383,9 @@ def tile_mamba3mimoblock_pa_kernel(
                 in_=wb_grouped[:],
             )
         steps["WB"] = weights_b
+        steps["W"] = weights_a
+        for i in CFG["first_w"]:
+            weights_a(i)
 
         def follow(slot, g):
             for step in PLAN.get((slot, g), []):
@@ -361,7 +399,7 @@ def tile_mamba3mimoblock_pa_kernel(
         sorted_words[0] = sort_words(0)
         for piece in range(PIECES):
             if piece + 1 < PIECES:
-                sorted_words[piece + 1] = sort_words(piece + 1)
-            grouped[piece] = (transposes_and_copies(None, PIECE_TILES, SCALAR_BANKS[piece], sorted_words[piece], piece))
+                sorted_words.setdefault(piece + 1, {}).update(sort_words(piece + 1))
+            transposes_and_copies(None, PIECE_TILES, SCALAR_BANKS[piece], sorted_words[piece], piece)
             follow(piece, 4)
         follow(PIECES, 0)

@@ -35,11 +35,13 @@ X_BUFFERS = 6
 PRODUCT_LAG = 1
 EXP_CAP = 2.0**60
 
-CFG = {"plan": {"0,4": "Q0","1,1": "VA0","1,4": "Q1 M0","2,0": "","2,4": "Q2","3,0": "M1","3,2": "EX0 TH0","3,4": "Q3 CAP0","4,0": "M2","4,4": "Q4","5,0": "M3","5,2": "EX1 TH1","5,4": "CAP1 Q5 LN0 LN1","6,0": "M4","6,3": "ST0 ST1 U0 RN0","6,4": "Q6","7,0": "M5","7,1": "EX2 TH2","7,2": "U1","7,3": "CAP2","7,4": "Q7","8,0": "M6 WB0 M7 DC0 DC1 RN1 FR0 FR1 EX3 TH3 CAP3 LN2 LN3 DS0 DS1 BV0 BV1 ST2 ST3 U2 U3 RN2 RN3 FR2 FR3 SN0 AB0 CS0 SN1 AB1 CS1 RS0 RC0 RA0 RS1 RC1 RA1 SN2 AB2 CS2 SN3 AB3 CS3 RS2 RC2 RA2 RS3 RC3 BV2 BV3 DMP0 DMP1 RA3 DC2 DC3 DMP2 DMP3","2,1": "VEC VS3","1,3": "VS2","3,1": "VS4","4,1": "VS5"},"sb": {"0": [1,3],"1": [1,2],"2": [0,2],"3": [0,2],"4": [0,2],"5": [0],"6": [0,1,2,3],"7": [0,2]},"wb": [[],[0,2]],"xt": [0,1,2,3],"zdt": [4,6,7,4],"zph": [5,5,5,5],"rowb": {"B0": 6,"B1": 0,"S0": 1,"C0": 2,"S1": 3,"C1": 7,"S2": 5,"C2": 4,"S3": 1,"C3": 2,"D0": 3,"D1": 7,"D2": 5,"D3": 4,"B2": 6,"B3": 0},"sort": [3],"gdamp": [],"cap": "vector","wdt_cuts": [[0,1024],[1024,2048]],"x0_cuts": [[0,1024],[1024,2048]],"wb_after": 7,"vadd": [],"cb": [0,1,2,3],"first_w": [0,1],"loads": [["w",0,0,2],["w",0,1,2],["w",1,0,1],["x",0,0,2],["x",0,1,2],["x",1,0,2],["x",1,1,2],["x",2,0,1],["x",3,0,1],["x",4,0,1],["x",5,0,1],["x",6,0,1],["x",7,0,1],["w",2,0,1]],"sortp": [[],[],[3],[3],[3],[3],[3],[3]],"vs": {"2": [[2,"s"]],"3": [[2,"s"]],"4": [[2,"s"]],"5": [[2,"s"]]}}
+CFG = {"plan": {"0,4": "Q0","1,1": "VA0","1,4": "Q1 M0","2,0": "","2,4": "Q2","3,0": "M1","3,2": "EX0 TH0 HF0","3,4": "Q3 CAP0","4,0": "M2","4,4": "Q4","5,0": "M3","5,2": "EX1 TH1 HF1","5,4": "CAP1 Q5 LN0 LN1","6,0": "M4","6,3": "ST0 ST1 U0 RG0","6,4": "Q6","7,0": "M5 FG0","7,1": "EX2 TH2 HF2","7,2": "","7,3": "CAP2","7,4": "Q7 U1","8,0": "M6 WB0 M7 DC0 DC1 RG1 FG1 EX3 TH3 HF3 CAP3 LN2 LN3 DS0 DS1 BV0 BV1 ST2 ST3 U2 U3 RG2 RG3 FG2 FG3 SN0 AB0 CS0 SN1 AB1 CS1 RS0 RC0 RA0 RS1 RC1 RA1 SN2 AB2 CS2 SN3 AB3 CS3 RS2 RC2 RA2 RS3 RC3 BV2 BV3 DMP0 DMP1 RA3 DC2 DC3 DMP2 DMP3","2,1": "VEC VS3","1,3": "VS2","3,1": "VS4","4,1": "VS5"},"sb": {"0": [1,3],"1": [1,2],"2": [0,2],"3": [0,2],"4": [0,2],"5": [0],"6": [0,1,2,3],"7": [0]},"wb": [[],[0,2]],"xt": [0,1,2,3],"zdt": [4,6,7,4],"zph": [5,5,5,5],"rowb": {"B0": 6,"B1": 0,"S0": 1,"C0": 2,"S1": 3,"C1": 7,"S2": 5,"C2": 4,"S3": 1,"C3": 2,"D0": 3,"D1": 7,"D2": 5,"D3": 4,"B2": 6,"B3": 0},"sort": [3],"gdamp": [],"cap": "vector","wdt_cuts": [[0,1024],[1024,2048]],"x0_cuts": [[0,1024],[1024,2048]],"wb_after": 7,"vadd": [],"cb": [0,1],"first_w": [0,1],"loads": [["w",0,0,2],["w",0,1,2],["w",1,0,1],["x",0,0,2],["x",0,1,2],["x",1,0,2],["x",1,1,2],["x",2,0,1],["x",3,0,1],["x",4,0,1],["x",5,0,1],["x",6,0,1],["x",7,0,1],["w",2,0,1]],"sortp": [[],[],[],[],[],[],[],[]],"vs": {"2": [[3,"s"],[2,"v"]],"3": [[3,"s"],[2,"v"]],"4": [[3,"s"],[2,"v"]],"5": [[3,"s"],[2,"v"]]},"unit": 2}
 PLAN = {tuple(int(v) for v in k.split(",")): v.split() for k, v in CFG["plan"].items()}
 SCALAR_BANKS = {int(k): tuple(v) for k, v in CFG["sb"].items()}
 W_BANKS = tuple(CFG["wb"])
 X_BUFFERS = 6
+ROUND_MAGIC = 1.5 * 2.0**23
+UNIT = CFG.get("unit", 1.0)
 WB_SLOT = 7
 BANKS = 8
 XT = tuple(CFG["xt"])
@@ -168,7 +170,7 @@ def tile_mamba3mimoblock_pa_kernel(
             nc.gpsimd.tensor_scalar(out=neg_a_col[:], in0=a_col[:], scalar1=-1.0, scalar2=0.0, op0=ALU.mult, op1=ALU.add)
             cols["neg_a"] = neg_a_col[:]
             half_turns_col = const.tile([P, 1], F32, name="half_turns_col")
-            nc.vector.tensor_scalar_mul(out=half_turns_col[:], in0=per_chan[:, 3:4], scalar1=1.0 / math.pi)
+            nc.vector.tensor_scalar_mul(out=half_turns_col[:], in0=per_chan[:, 3:4], scalar1=1.0 / (math.pi * UNIT))
             cols["half_turns"] = half_turns_col[:]
             cols["scratch"] = const.tile([P, 1], F32, name="scratch")[:]
 
@@ -283,6 +285,21 @@ def tile_mamba3mimoblock_pa_kernel(
                 out=turn[c][:], in0=soft[c][:], scalar=cols["half_turns"], in1=turn[c][:], op0=ALU.mult, op1=ALU.add
             )
 
+        def halve_tanh(c):
+            nc.gpsimd.tensor_scalar(
+                out=turn[c][:], in0=turn[c][:], scalar1=0.5, scalar2=0.0, op0=ALU.mult, op1=ALU.add
+            )
+
+        def nearest_turn(c):
+            turns[c] = chan3.tile([P, CHUNK_COLS], F32, name="turns", tag="turns")
+            nc.vector.tensor_scalar(
+                out=turns[c][:], in0=turn[c][:], scalar1=ROUND_MAGIC, scalar2=ROUND_MAGIC, op0=ALU.add, op1=ALU.subtract
+            )
+
+        def fraction_g(c):
+            frac[c] = turn[c]
+            nc.gpsimd.tensor_sub(out=frac[c][:], in0=turns[c][:], in1=turn[c][:])
+
         def nearest_even(c):
             turns[c] = chan3.tile([P, CHUNK_COLS], I32, name="turns", tag="turns")
             nc.vector.tensor_scalar_mul(out=turns[c][:], in0=turn[c][:], scalar1=0.5)
@@ -298,7 +315,7 @@ def tile_mamba3mimoblock_pa_kernel(
 
         def sine_of(c):
             sine[c] = chan3.tile([P, CHUNK_COLS], F32, name="sine", tag="sine")
-            nc.scalar.activation(out=sine[c][:], in_=frac[c][:], func=ACT.Sin, scale=-math.pi)
+            nc.scalar.activation(out=sine[c][:], in_=frac[c][:], func=ACT.Sin, scale=-math.pi * UNIT)
 
         def magnitude_of(c):
             cosine[c] = chan3.tile([P, CHUNK_COLS], F32, name="cosine", tag="cosine")
@@ -306,7 +323,7 @@ def tile_mamba3mimoblock_pa_kernel(
 
         def cosine_of(c):
             nc.scalar.activation(
-                out=cosine[c][:], in_=cosine[c][:], func=ACT.Sin, scale=-math.pi, bias=math.pi / 2.0
+                out=cosine[c][:], in_=cosine[c][:], func=ACT.Sin, scale=-math.pi * UNIT, bias=math.pi / 2.0
             )
 
         def decay(c):
@@ -365,7 +382,7 @@ def tile_mamba3mimoblock_pa_kernel(
 
         steps = {
             "EX": exp_of, "TH": tanh_of, "CAP": cap, "LN": logarithm, "ST": step_size, "U": angle, "RN": nearest_even,
-            "FR": fraction, "SN": sine_of, "TT": silu_table, "AB": magnitude_of, "CS": cosine_of, "DC": decay, "BV": b_val, "RS": rot_sin, "RC": rot_cos, "RA": rot_add, "DS": damp_state,
+            "FR": fraction, "SN": sine_of, "HF": halve_tanh, "RG": nearest_turn, "FG": fraction_g, "TT": silu_table, "AB": magnitude_of, "CS": cosine_of, "DC": decay, "BV": b_val, "RS": rot_sin, "RC": rot_cos, "RA": rot_add, "DS": damp_state,
             "DMP": damp_and_store,
         }
 

@@ -35,7 +35,7 @@ X_BUFFERS = 6
 PRODUCT_LAG = 1
 EXP_CAP = 2.0**60
 
-CFG = {"plan": {"0,4": "Q0","1,1": "VA0","1,4": "Q1 M0","2,0": "","2,4": "Q2","3,0": "M1","3,2": "EX0 TH0 HF0","3,4": "Q3 CAP0","4,0": "M2","4,4": "Q4","5,0": "M3","5,2": "EX1 TH1 HF1","5,4": "CAP1 Q5 LN0 LN1","6,0": "M4","6,3": "ST0 ST1 U0 RG0","6,4": "Q6","7,0": "M5 FG0","7,1": "EX2 TH2 HF2","7,2": "","7,3": "CAP2","7,4": "Q7 U1","8,0": "M6 WB0 M7 DC0 DC1 RG1 FG1 EX3 TH3 HF3 CAP3 LN2 LN3 DS0 DS1 BV0 BV1 ST2 ST3 U2 U3 RG2 RG3 FG2 FG3 SN0 AB0 CS0 SN1 AB1 CS1 RS0 RC0 RA0 RS1 RC1 RA1 SN2 AB2 CS2 SN3 AB3 CS3 RS2 RC2 RA2 RS3 RC3 BV2 BV3 DMP0 DMP1 RA3 DC2 DC3 DMP2 DMP3","2,1": "VEC VS3","1,3": "VS2","3,1": "VS4","4,1": "VS5"},"sb": {"0": [1,3],"1": [1,2],"2": [0,2],"3": [0,2],"4": [0,2],"5": [0],"6": [0,1,2,3],"7": [0]},"wb": [[],[0,2]],"xt": [0,1,2,3],"zdt": [4,6,7,4],"zph": [5,5,5,5],"rowb": {"B0": 6,"B1": 0,"S0": 1,"C0": 2,"S1": 3,"C1": 7,"S2": 5,"C2": 4,"S3": 1,"C3": 2,"D0": 3,"D1": 7,"D2": 5,"D3": 4,"B2": 6,"B3": 0},"sort": [3],"gdamp": [],"cap": "vector","wdt_cuts": [[0,1024],[1024,2048]],"x0_cuts": [[0,1024],[1024,2048]],"wb_after": 7,"vadd": [],"cb": [0,1],"first_w": [0,1],"loads": [["w",0,0,2],["w",0,1,2],["w",1,0,1],["x",0,0,2],["x",0,1,2],["x",1,0,2],["x",1,1,2],["x",2,0,1],["x",3,0,1],["x",4,0,1],["x",5,0,1],["x",6,0,1],["x",7,0,1],["w",2,0,1]],"sortp": [[],[],[],[],[],[],[],[]],"vs": {"2": [[3,"s"],[2,"v"]],"3": [[3,"s"],[2,"v"]],"4": [[3,"s"],[2,"v"]],"5": [[3,"s"],[2,"v"]]},"unit": 2}
+CFG = {"plan": {"0,4": "Q0","1,1": "VA0","1,4": "Q1 M0","2,0": "","2,4": "Q2","3,0": "M1","3,2": "EX0 TH0 HF0","3,4": "Q3 CAP0","4,0": "M2","4,4": "Q4","5,0": "M3","5,2": "EX1 TH1 HF1","5,4": "CAP1 Q5 LN0 LN1","6,0": "M4","6,3": "ST0 ST1 U0 RG0","6,4": "Q6","7,0": "M5 FG0","7,1": "EX2 TH2 HF2","7,2": "","7,3": "CAP2","7,4": "Q7 U1","8,0": "M6 WB0 M7 DC0 DC1 RG1 FG1 EX3 TH3 HF3 CAP3 LN2 LN3 DS0 DS1 BV0 BV1 BV2 BV3 ST2 ST3 U2 U3 RG2 RG3 FG2 FG3 SN0 AB0 CS0 SN1 AB1 CS1 RS0 RC0 RA0 RS1 RC1 RA1 SN2 AB2 CS2 SN3 AB3 CS3 RS2 RC2 RA2 RS3 RC3 DMP0 DMP1 RA3 DC2 DC3 DMP2 DMP3","2,1": "VEC VS3","1,3": "VS2","3,1": "VS4","4,1": "VS5"},"sb": {"0": [1,3],"1": [1,2],"2": [0,2],"3": [0,2],"4": [0,2],"5": [0],"6": [0,1,2,3],"7": [0]},"wb": [[],[0,2]],"xt": [0,1,2,3],"zdt": [4,6,7,4],"zph": [5,5,5,5],"rowb": {"B0": 6,"B1": 0,"S0": 1,"C0": 2,"S1": 3,"C1": 7,"S2": 5,"C2": 4,"S3": 1,"C3": 2,"D0": 3,"D1": 7,"D2": 5,"D3": 4,"B2": 6,"B3": 0},"sort": [3],"gdamp": [],"cap": "vector","wdt_cuts": [[0,1024],[1024,2048]],"x0_cuts": [[0,1024],[1024,2048]],"wb_after": 7,"vadd": [],"cb": [0,1],"first_w": [0,1],"loads": [["w",0,0,2],["w",0,1,2],["w",1,0,1],["x",0,0,2],["x",0,1,2],["x",1,0,2],["x",1,1,2],["x",2,0,1],["x",3,0,1],["x",4,0,1],["x",5,0,1],["x",6,0,1],["x",7,0,1],["w",2,0,1]],"sortp": [[],[],[],[],[],[],[],[]],"vs": {"2": [[3,"s"],[2,"v"]],"3": [[3,"s"],[2,"v"]],"4": [[3,"s"],[2,"v"]],"5": [[3,"s"],[2,"v"]]},"unit": 2}
 PLAN = {tuple(int(v) for v in k.split(",")): v.split() for k, v in CFG["plan"].items()}
 SCALAR_BANKS = {int(k): tuple(v) for k, v in CFG["sb"].items()}
 W_BANKS = tuple(CFG["wb"])
@@ -219,14 +219,34 @@ def tile_mamba3mimoblock_pa_kernel(
                 in_=grouped[piece][:, half * width : (half + 1) * width],
             )
 
-        def products(piece):
+        def products_half(piece, passes):
             c = piece // PIECES_PER_CHUNK
             half = piece % PIECES_PER_CHUNK
-            if half == 0:
+            if c not in z_dt:
+                z_dt[c] = bank_tile([P, CHUNK_COLS], 0)
+                z_ph[c] = bank_tile([P, CHUNK_COLS], 0)
+            cols_ = slice(half * PIECE_COLS, (half + 1) * PIECE_COLS)
+            for g in passes:
+                for i, z in enumerate((z_dt[c], z_ph[c])):
+                    nc.tensor.matmul_mx(
+                        out=z[:, cols_],
+                        lhsT=w2_codes[:, i, g, :].bitcast(FP8X4),
+                        lhsT_scale=w2_scales[:, i, g, :],
+                        rhs=x_codes[:, piece, g].rearrange("q j p -> q (j p)").bitcast(FP8X4),
+                        rhs_scale=x_scales[:, piece, g].rearrange("q j p -> q (j p)"),
+                        start=(g == 0),
+                        stop=(g == PASSES - 1),
+                    )
+
+        def products(piece, which=(0, 1)):
+            c = piece // PIECES_PER_CHUNK
+            half = piece % PIECES_PER_CHUNK
+            if half == 0 and c not in z_dt:
                 z_dt[c] = bank_tile([P, CHUNK_COLS], ZDT[c])
                 z_ph[c] = bank_tile([P, CHUNK_COLS], ZPH[c])
             cols = slice(half * PIECE_COLS, (half + 1) * PIECE_COLS)
-            for i, z in enumerate((z_dt[c], z_ph[c])):
+            for i in which:
+                z = (z_dt[c], z_ph[c])[i]
                 for g in range(PASSES):
                     nc.tensor.matmul_mx(
                         out=z[:, cols],
@@ -300,6 +320,13 @@ def tile_mamba3mimoblock_pa_kernel(
             frac[c] = turn[c]
             nc.gpsimd.tensor_sub(out=frac[c][:], in0=turns[c][:], in1=turn[c][:])
 
+        def fraction_v(c):
+            frac[c] = turn[c]
+            nc.vector.tensor_sub(out=frac[c][:], in0=turns[c][:], in1=turn[c][:])
+
+        def halve_tanh_v(c):
+            nc.vector.tensor_scalar_mul(out=turn[c][:], in0=turn[c][:], scalar1=0.5)
+
         def nearest_even(c):
             turns[c] = chan3.tile([P, CHUNK_COLS], I32, name="turns", tag="turns")
             nc.vector.tensor_scalar_mul(out=turns[c][:], in0=turn[c][:], scalar1=0.5)
@@ -338,7 +365,7 @@ def tile_mamba3mimoblock_pa_kernel(
         def both(bank):
             return bank[:].rearrange("p t r -> p (t r)").unsqueeze(1).broadcast_to([P, 2, CHUNK_COLS])
 
-        by_sin, by_cos, damped = {}, {}, {}
+        by_sin, by_cos, damped, decay_banks = {}, {}, {}, {}
 
         def damp_state(c):
             t0 = c * CHUNK_TILES
@@ -364,6 +391,27 @@ def tile_mamba3mimoblock_pa_kernel(
             eng.tensor_sub(out=parts[c][:, 0], in0=by_cos[c][:, 0], in1=by_sin[c][:, 1])
             eng.tensor_add(out=parts[c][:, 1], in0=by_cos[c][:, 1], in1=by_sin[c][:, 0])
 
+        def damp_im(c):
+            t0 = c * CHUNK_TILES
+            if c not in damped:
+                nc.vector.tensor_mul(out=parts[c][:, 1], in0=parts[c][:, 1], in1=decay_banks[c][:].rearrange("p t r -> p (t r)"))
+            nc.sync.dma_start(out=im_rows[:, t0 : t0 + CHUNK_TILES, :], in_=parts[c][:, 1].rearrange("p (t r) -> p t r", r=R))
+
+        def damp_re(c):
+            decay_banks[c] = back_to_rows(soft[c], "D%d" % c)
+            nc.vector.tensor_mul(out=parts[c][:, 0], in0=parts[c][:, 0], in1=decay_banks[c][:].rearrange("p t r -> p (t r)"))
+
+        def damp_both(c):
+            t0 = c * CHUNK_TILES
+            decay_banks[c] = back_to_rows(soft[c], "D%d" % c)
+            nc.vector.tensor_mul(out=parts[c][:], in0=parts[c][:], in1=both(decay_banks[c]))
+            nc.sync.dma_start(out=im_rows[:, t0 : t0 + CHUNK_TILES, :], in_=parts[c][:, 1].rearrange("p (t r) -> p t r", r=R))
+
+        def add_b(c):
+            t0 = c * CHUNK_TILES
+            nc.vector.tensor_add(out=parts[c][:, 0], in0=parts[c][:, 0], in1=z_b[c][:].rearrange("p t r -> p (t r)"))
+            nc.sync.dma_start(out=re_rows[:, t0 : t0 + CHUNK_TILES, :], in_=parts[c][:, 0].rearrange("p (t r) -> p t r", r=R))
+
         def damp_and_store(c):
             t0 = c * CHUNK_TILES
             decay_t = None if c in damped else back_to_rows(soft[c], "D%d" % c)
@@ -382,13 +430,17 @@ def tile_mamba3mimoblock_pa_kernel(
 
         steps = {
             "EX": exp_of, "TH": tanh_of, "CAP": cap, "LN": logarithm, "ST": step_size, "U": angle, "RN": nearest_even,
-            "FR": fraction, "SN": sine_of, "HF": halve_tanh, "RG": nearest_turn, "FG": fraction_g, "TT": silu_table, "AB": magnitude_of, "CS": cosine_of, "DC": decay, "BV": b_val, "RS": rot_sin, "RC": rot_cos, "RA": rot_add, "DS": damp_state,
+            "FR": fraction, "SN": sine_of, "DI": damp_im, "DR": damp_re, "DB": damp_both, "BA": add_b, "HF": halve_tanh, "RG": nearest_turn, "FG": fraction_g, "FV": fraction_v, "HV": halve_tanh_v, "TT": silu_table, "AB": magnitude_of, "CS": cosine_of, "DC": decay, "BV": b_val, "RS": rot_sin, "RC": rot_cos, "RA": rot_add, "DS": damp_state,
             "DMP": damp_and_store,
         }
 
         sorted_words = {}
         steps["M"] = products
         steps["VS"] = vector_sort
+        steps["MA"] = lambda c: products_half(c, (0, 1))
+        steps["MZ"] = lambda c: products_half(c, (2, 3))
+        steps["MD"] = lambda c: products(c, (0,))
+        steps["MP"] = lambda c: products(c, (1,))
         steps["QA"] = lambda c: quantise_half(c, 0)
         steps["QZ"] = lambda c: quantise_half(c, 1)
         steps["Q"] = lambda c: quantise(c, grouped[c])

@@ -35,11 +35,11 @@ X_BUFFERS = 6
 PRODUCT_LAG = 1
 EXP_CAP = 2.0**60
 
-CFG = {"plan": {"0,4": "Q0","1,1": "VA0","1,4": "Q1 M0","2,0": "","2,4": "Q2","3,0": "M1","3,2": "EX0 TH0 HF0","3,4": "Q3 CAP0","4,0": "M2","4,4": "Q4","5,0": "M3","5,2": "EX1 TH1 HF1","5,4": "CAP1 Q5 LN0 LN1","6,0": "M4","6,3": "ST0 ST1 U0 RG0","6,4": "Q6","7,0": "M5 FG0","7,1": "EX2 TH2 HF2","7,2": "","7,3": "CAP2","7,4": "Q7 U1","8,0": "M6 WB0 M7 DC0 DC1 RG1 FG1 EX3 TH3 HF3 CAP3 LN2 LN3 DS0 DS1 BV0 BV1 BV2 BV3 ST2 ST3 U2 U3 RG2 RG3 FG2 FG3 SN0 AB0 CS0 SN1 AB1 CS1 RS0 RC0 RA0 RS1 RC1 RA1 SN2 AB2 CS2 SN3 AB3 CS3 RS2 RC2 RA2 RS3 RC3 DMP0 DMP1 RA3 DC2 DC3 DMP2 DMP3","2,1": "VEC VS3","1,3": "VS2","3,1": "VS4","4,1": "VS5"},"sb": {"0": [1,3],"1": [1,2],"2": [0,2],"3": [0,2],"4": [0,2],"5": [0],"6": [0,1,2,3],"7": [0]},"wb": [[],[0,2]],"xt": [0,1,2,3],"zdt": [4,6,7,4],"zph": [5,5,5,5],"rowb": {"B0": 6,"B1": 0,"S0": 1,"C0": 2,"S1": 3,"C1": 7,"S2": 5,"C2": 4,"S3": 1,"C3": 2,"D0": 3,"D1": 7,"D2": 5,"D3": 4,"B2": 6,"B3": 0},"sort": [3],"gdamp": [],"cap": "vector","wdt_cuts": [[0,1024],[1024,2048]],"x0_cuts": [[0,1024],[1024,2048]],"wb_after": 7,"vadd": [],"cb": [0,1],"first_w": [0,1],"loads": [["w",0,0,2],["w",0,1,2],["w",1,0,1],["x",0,0,2],["x",0,1,2],["x",1,0,2],["x",1,1,2],["x",2,0,1],["x",3,0,1],["x",4,0,1],["x",5,0,1],["x",6,0,1],["x",7,0,1],["w",2,0,1]],"sortp": [[],[],[],[],[],[],[],[]],"vs": {"2": [[3,"s"],[2,"v"]],"3": [[3,"s"],[2,"v"]],"4": [[3,"s"],[2,"v"]],"5": [[3,"s"],[2,"v"]]},"unit": 2}
+CFG = {"plan": {"0,4": "Q0","1,1": "VA0","1,4": "MD0 Q1","2,0": "MP0","2,4": "Q2","3,0": "M1","3,2": "EX0 TH0 HF0","3,4": "Q3 CAP0","4,0": "M2","4,4": "Q4","5,0": "M3","5,2": "EX1 TH1 HF1","5,4": "CAP1 Q5 LN0 LN1","6,0": "MP4","6,3": "MD5 ST0 ST1 U0 RG0","6,4": "Q6","7,0": "MP5 FG0","7,1": "EX2 TH2 HF2","7,2": "","7,3": "CAP2","7,4": "Q7 U1","8,0": "M6 WB0 M7 DC0 DC1 RG1 FG1 EX3 TH3 HF3 CAP3 LN2 LN3 DS0 DS1 BV0 BV1 BV2 BV3 ST2 ST3 U2 U3 RG2 RG3 FG2 FG3 SN0 AB0 CS0 SN1 AB1 CS1 RS0 RC0 RA0 RS1 RC1 RA1 SN2 AB2 CS2 SN3 AB3 CS3 RS2 RC2 RI2 RS3 RC3 DI0 DI1 RV2 RA3 DC2 DC3 DB2 BA0 BA2 DR3 DI3 BA1 BA3","2,1": "VEC VS3","1,3": "VS2","3,1": "VS4","4,1": "VS5","5,3": "MD4"},"sb": {"0": [1,3],"1": [1,2],"2": [0,1,2],"3": [0,1,2],"4": [0,1,2],"5": [0],"6": [0,1,2,3],"7": [0]},"wb": [[],[0,2]],"xt": [0,1,2,3],"zdt": [4,6,7,4],"zph": [5,5,5,5],"rowb": {"B0": 6,"B1": 0,"S0": 1,"C0": 2,"S1": 3,"C1": 7,"S2": 5,"C2": 4,"S3": 1,"C3": 2,"D0": 3,"D1": 7,"D2": 5,"D3": 4,"B2": 6,"B3": 0},"sort": [3],"gdamp": [],"cap": "vector","wdt_cuts": [[0,1024],[1024,2048]],"x0_cuts": [[0,1024],[1024,2048]],"wb_after": 7,"vadd": [],"cb": [0,1],"first_w": [0,1],"loads": [["w",0,0,2],["w",0,1,2],["w",1,0,1],["x",0,0,2],["x",0,1,2],["x",1,0,2],["x",1,1,2],["x",2,0,1],["x",3,0,1],["x",4,0,1],["x",5,0,1],["x",6,0,1],["x",7,0,1],["w",2,0,1]],"sortp": [[],[],[],[],[],[],[],[]],"vs": {"2": [[3,"v"],[2,"v"],[1,"s"]],"3": [[3,"v"],[2,"v"],[1,"s"]],"4": [[3,"v"],[2,"v"],[1,"s"]],"5": [[3,"v"],[2,"v"],[1,"s"]]},"unit": 2}
 PLAN = {tuple(int(v) for v in k.split(",")): v.split() for k, v in CFG["plan"].items()}
 SCALAR_BANKS = {int(k): tuple(v) for k, v in CFG["sb"].items()}
 W_BANKS = tuple(CFG["wb"])
-X_BUFFERS = 6
+X_BUFFERS = 5
 ROUND_MAGIC = 1.5 * 2.0**23
 UNIT = CFG.get("unit", 1.0)
 WB_SLOT = 7
@@ -63,7 +63,7 @@ def tile_mamba3mimoblock_pa_kernel(
         xpool = ctx.enter_context(tc.tile_pool(name="xpool", bufs=X_BUFFERS))
         stage = ctx.enter_context(tc.tile_pool(name="stage", bufs=3))
         keep = ctx.enter_context(tc.tile_pool(name="keep", bufs=1))
-        chan = ctx.enter_context(tc.tile_pool(name="chan", bufs=CHUNKS))
+        chan2 = ctx.enter_context(tc.tile_pool(name="chan2", bufs=2))
         chan3 = ctx.enter_context(tc.tile_pool(name="chan3", bufs=3))
         rows = ctx.enter_context(tc.tile_pool(name="rows", bufs=CHUNKS))
         rows3 = ctx.enter_context(tc.tile_pool(name="rows3", bufs=3))
@@ -177,6 +177,7 @@ def tile_mamba3mimoblock_pa_kernel(
         grouped = {}
         x_codes = keep.tile([P, PIECES, PASSES, PIECE_TILES, P], U32, align_bytes=64)
         x_scales = keep.tile([P, PIECES, PASSES, PIECE_TILES, P], U8, align_bytes=64)
+        soft_pair, turn_pair, turns_pair, decay_tile = {}, {}, {}, {}
         turns, z_dt, z_ph, z_b, soft, turn, frac, sine, cosine, parts = {}, {}, {}, {}, {}, {}, {}, {}, {}, {}
 
         def pass_of(piece, g):
@@ -194,6 +195,12 @@ def tile_mamba3mimoblock_pa_kernel(
             return out
 
         def vector_sort(piece):
+            if CFG.get("merge") and len(CFG["vs"][str(piece)]) == 2:
+                by_parity = stage.tile([P, 2, PIECE_TILES, 2, P], F32, name="by_parity2", tag="by_parity2", bufs=3)
+                words = x_sb[piece][:].bitcast(F32)[:, 0, :, 2 * WORDS_PASS : 4 * WORDS_PASS]
+                nc.vector.tensor_copy(out=by_parity[:], in_=words.rearrange("p j (g q u) -> p g j u q", g=2, u=2))
+                sorted_words.setdefault(piece, {}).update({2: by_parity[:, 0], 3: by_parity[:, 1]})
+                return
             for g, eng in CFG["vs"][str(piece)]:
                 by_parity = stage.tile([P, PIECE_TILES, 2, P], F32, name="by_parity", tag="by_parity", bufs=6)
                 src = pass_of(piece, g).rearrange("p j (q u) -> p j u q", u=2)
@@ -259,21 +266,25 @@ def tile_mamba3mimoblock_pa_kernel(
                     )
 
         def exp_of(c):
-            soft[c] = chan.tile([P, CHUNK_COLS], F32, name="soft", tag="soft")
-            nc.scalar.activation(out=soft[c][:], in_=z_dt[c][:], func=ACT.Exp, bias=cols["b_dt"], scale=1.0)
+            if c % 2 == 0:
+                soft_pair[c // 2] = chan2.tile([P, 2, CHUNK_COLS], F32, name="soft", tag="soft")
+            soft[c] = soft_pair[c // 2][:, c % 2]
+            nc.scalar.activation(out=soft[c], in_=z_dt[c][:], func=ACT.Exp, bias=cols["b_dt"], scale=1.0)
 
         def tanh_of(c):
-            turn[c] = chan.tile([P, CHUNK_COLS], F32, name="turn", tag="turn")
-            nc.scalar.activation(out=turn[c][:], in_=z_ph[c][:], func=ACT.Tanh, bias=cols["b_ph"], scale=1.0)
+            if c % 2 == 0:
+                turn_pair[c // 2] = chan2.tile([P, 2, CHUNK_COLS], F32, name="turn", tag="turn")
+            turn[c] = turn_pair[c // 2][:, c % 2]
+            nc.scalar.activation(out=turn[c], in_=z_ph[c][:], func=ACT.Tanh, bias=cols["b_ph"], scale=1.0)
 
         def cap(c):
             if CAP_ENGINE == "gpsimd":
                 nc.gpsimd.tensor_scalar(
-                    out=soft[c][:], in0=soft[c][:], scalar1=EXP_CAP, scalar2=1.0, op0=ALU.min, op1=ALU.add
+                    out=soft[c], in0=soft[c], scalar1=EXP_CAP, scalar2=1.0, op0=ALU.min, op1=ALU.add
                 )
             else:
                 nc.vector.tensor_scalar(
-                    out=soft[c][:], in0=soft[c][:], scalar1=EXP_CAP, scalar2=1.0, op0=ALU.min, op1=ALU.add
+                    out=soft[c], in0=soft[c], scalar1=EXP_CAP, scalar2=1.0, op0=ALU.min, op1=ALU.add
                 )
 
         def b_val(c):
@@ -293,68 +304,99 @@ def tile_mamba3mimoblock_pa_kernel(
                     )
 
         def logarithm(c):
-            nc.scalar.activation(out=soft[c][:], in_=soft[c][:], func=ACT.Ln)
+            nc.scalar.activation(out=soft[c], in_=soft[c], func=ACT.Ln)
 
         def step_size(c):
             nc.vector.scalar_tensor_tensor(
-                out=soft[c][:], in0=z_dt[c][:], scalar=cols["b_dt"], in1=soft[c][:], op0=ALU.add, op1=ALU.max
+                out=soft[c], in0=z_dt[c][:], scalar=cols["b_dt"], in1=soft[c], op0=ALU.add, op1=ALU.max
             )
 
         def angle(c):
             nc.vector.scalar_tensor_tensor(
-                out=turn[c][:], in0=soft[c][:], scalar=cols["half_turns"], in1=turn[c][:], op0=ALU.mult, op1=ALU.add
+                out=turn[c], in0=soft[c], scalar=cols["half_turns"], in1=turn[c], op0=ALU.mult, op1=ALU.add
             )
 
         def halve_tanh(c):
             nc.gpsimd.tensor_scalar(
-                out=turn[c][:], in0=turn[c][:], scalar1=0.5, scalar2=0.0, op0=ALU.mult, op1=ALU.add
+                out=turn[c], in0=turn[c], scalar1=0.5, scalar2=0.0, op0=ALU.mult, op1=ALU.add
             )
 
         def nearest_turn(c):
-            turns[c] = chan3.tile([P, CHUNK_COLS], F32, name="turns", tag="turns")
+            if c % 2 == 0:
+                turns_pair[c // 2] = chan2.tile([P, 2, CHUNK_COLS], F32, name="turns", tag="turns")
+            turns[c] = turns_pair[c // 2][:, c % 2]
             nc.vector.tensor_scalar(
-                out=turns[c][:], in0=turn[c][:], scalar1=ROUND_MAGIC, scalar2=ROUND_MAGIC, op0=ALU.add, op1=ALU.subtract
+                out=turns[c], in0=turn[c], scalar1=ROUND_MAGIC, scalar2=ROUND_MAGIC, op0=ALU.add, op1=ALU.subtract
             )
 
         def fraction_g(c):
             frac[c] = turn[c]
-            nc.gpsimd.tensor_sub(out=frac[c][:], in0=turns[c][:], in1=turn[c][:])
+            nc.gpsimd.tensor_sub(out=frac[c], in0=turns[c], in1=turn[c])
 
         def fraction_v(c):
             frac[c] = turn[c]
-            nc.vector.tensor_sub(out=frac[c][:], in0=turns[c][:], in1=turn[c][:])
+            nc.vector.tensor_sub(out=frac[c], in0=turns[c], in1=turn[c])
 
         def halve_tanh_v(c):
-            nc.vector.tensor_scalar_mul(out=turn[c][:], in0=turn[c][:], scalar1=0.5)
-
-        def nearest_even(c):
-            turns[c] = chan3.tile([P, CHUNK_COLS], I32, name="turns", tag="turns")
-            nc.vector.tensor_scalar_mul(out=turns[c][:], in0=turn[c][:], scalar1=0.5)
-
-        def fraction(c):
-            frac[c] = turn[c]
-            nc.vector.scalar_tensor_tensor(
-                out=frac[c][:], in0=turns[c][:], scalar=2.0, in1=turn[c][:], op0=ALU.mult, op1=ALU.subtract
-            )
+            nc.vector.tensor_scalar_mul(out=turn[c], in0=turn[c], scalar1=0.5)
 
         def silu_table(c):
             nc.scalar.activation(out=cols["scratch"], in_=cols["b_dt"], func=ACT.Silu)
 
         def sine_of(c):
             sine[c] = chan3.tile([P, CHUNK_COLS], F32, name="sine", tag="sine")
-            nc.scalar.activation(out=sine[c][:], in_=frac[c][:], func=ACT.Sin, scale=-math.pi * UNIT)
+            nc.scalar.activation(out=sine[c][:], in_=frac[c], func=ACT.Sin, scale=-math.pi * UNIT)
 
         def magnitude_of(c):
             cosine[c] = chan3.tile([P, CHUNK_COLS], F32, name="cosine", tag="cosine")
-            nc.scalar.activation(out=cosine[c][:], in_=frac[c][:], func=ACT.Abs)
+            nc.scalar.activation(out=cosine[c][:], in_=frac[c], func=ACT.Abs)
 
         def cosine_of(c):
             nc.scalar.activation(
                 out=cosine[c][:], in_=cosine[c][:], func=ACT.Sin, scale=-math.pi * UNIT, bias=math.pi / 2.0
             )
 
+        decays = {}
+
+        def decay_pair_of(h):
+            both_chunks = chan2.tile([P, 2, CHUNK_COLS], F32, name="decay", tag="decay")
+            nc.scalar.activation(out=both_chunks[:], in_=soft_pair[h][:], func=ACT.Exp, scale=cols["neg_a"])
+            for i in range(2):
+                decays[2 * h + i] = both_chunks[:, i]
+
         def decay(c):
-            nc.scalar.activation(out=soft[c][:], in_=soft[c][:], func=ACT.Exp, scale=cols["neg_a"])
+            if c % 2 == 0:
+                decay_tile[c // 2] = chan2.tile([P, 2, CHUNK_COLS], F32, name="decay", tag="decay")
+            decays[c] = decay_tile[c // 2][:, c % 2]
+            nc.scalar.activation(out=decays[c], in_=soft[c], func=ACT.Exp, scale=cols["neg_a"])
+
+        def angle_on_gpsimd(c):
+            product = chan3.tile([P, CHUNK_COLS], F32, name="product", tag="product")
+            nc.gpsimd.tensor_scalar(
+                out=product[:], in0=soft[c], scalar1=cols["half_turns"], scalar2=0.0, op0=ALU.mult, op1=ALU.add
+            )
+            nc.gpsimd.tensor_add(out=turn[c], in0=product[:], in1=turn[c])
+
+        def angle_pair(h):
+            nc.vector.scalar_tensor_tensor(
+                out=turn_pair[h][:], in0=soft_pair[h][:], scalar=cols["half_turns"], in1=turn_pair[h][:], op0=ALU.mult, op1=ALU.add
+            )
+
+        def nearest_pair(h):
+            turns_pair[h] = chan2.tile([P, 2, CHUNK_COLS], F32, name="turns", tag="turns")
+            nc.vector.tensor_scalar(
+                out=turns_pair[h][:], in0=turn_pair[h][:], scalar1=ROUND_MAGIC, scalar2=ROUND_MAGIC, op0=ALU.add, op1=ALU.subtract
+            )
+            for i in range(2):
+                turns[2 * h + i] = turns_pair[h][:, i]
+
+        def cap_pair(h):
+            nc.vector.tensor_scalar(
+                out=soft_pair[h][:], in0=soft_pair[h][:], scalar1=EXP_CAP, scalar2=1.0, op0=ALU.min, op1=ALU.add
+            )
+
+        def log_pair(h):
+            nc.scalar.activation(out=soft_pair[h][:], in_=soft_pair[h][:], func=ACT.Ln)
 
         def back_to_rows(channel_tile, which):
             bank = bank_tile([P, CHUNK_TILES, R], ROWB[which])
@@ -367,11 +409,19 @@ def tile_mamba3mimoblock_pa_kernel(
 
         by_sin, by_cos, damped, decay_banks = {}, {}, {}, {}
 
+        def damp_state_half(c, i):
+            t0 = c * CHUNK_TILES
+            if i == 0:
+                damped[c] = rows2.tile([P, 2, CHUNK_COLS], F32, name="damped", tag="damped")
+                decay_banks[c] = back_to_rows(decays[c], "D%d" % c)
+            st = state[:, i, t0 : t0 + CHUNK_TILES, :].rearrange("p t r -> p (t r)")
+            nc.vector.tensor_mul(out=damped[c][:, i], in0=st, in1=decay_banks[c][:].rearrange("p t r -> p (t r)"))
+
         def damp_state(c):
             t0 = c * CHUNK_TILES
             st = state[:, :, t0 : t0 + CHUNK_TILES, :].rearrange("p c t r -> p c (t r)")
             damped[c] = rows2.tile([P, 2, CHUNK_COLS], F32, name="damped", tag="damped")
-            nc.vector.tensor_mul(out=damped[c][:], in0=st, in1=both(back_to_rows(soft[c], "D%d" % c)))
+            nc.vector.tensor_mul(out=damped[c][:], in0=st, in1=both(back_to_rows(decays[c], "D%d" % c)))
 
         def rot_sin(c):
             t0 = c * CHUNK_TILES
@@ -391,6 +441,14 @@ def tile_mamba3mimoblock_pa_kernel(
             eng.tensor_sub(out=parts[c][:, 0], in0=by_cos[c][:, 0], in1=by_sin[c][:, 1])
             eng.tensor_add(out=parts[c][:, 1], in0=by_cos[c][:, 1], in1=by_sin[c][:, 0])
 
+        def turned_re_on_vector(c):
+            parts[c] = by_cos[c]
+            nc.vector.tensor_sub(out=parts[c][:, 0], in0=by_cos[c][:, 0], in1=by_sin[c][:, 1])
+
+        def turned_im(c):
+            parts[c] = by_cos[c]
+            nc.gpsimd.tensor_add(out=parts[c][:, 1], in0=by_cos[c][:, 1], in1=by_sin[c][:, 0])
+
         def damp_im(c):
             t0 = c * CHUNK_TILES
             if c not in damped:
@@ -398,14 +456,30 @@ def tile_mamba3mimoblock_pa_kernel(
             nc.sync.dma_start(out=im_rows[:, t0 : t0 + CHUNK_TILES, :], in_=parts[c][:, 1].rearrange("p (t r) -> p t r", r=R))
 
         def damp_re(c):
-            decay_banks[c] = back_to_rows(soft[c], "D%d" % c)
+            decay_banks[c] = back_to_rows(decays[c], "D%d" % c)
             nc.vector.tensor_mul(out=parts[c][:, 0], in0=parts[c][:, 0], in1=decay_banks[c][:].rearrange("p t r -> p (t r)"))
 
         def damp_both(c):
             t0 = c * CHUNK_TILES
-            decay_banks[c] = back_to_rows(soft[c], "D%d" % c)
+            decay_banks[c] = back_to_rows(decays[c], "D%d" % c)
             nc.vector.tensor_mul(out=parts[c][:], in0=parts[c][:], in1=both(decay_banks[c]))
             nc.sync.dma_start(out=im_rows[:, t0 : t0 + CHUNK_TILES, :], in_=parts[c][:, 1].rearrange("p (t r) -> p t r", r=R))
+
+        b_rows, sums = {}, {}
+
+        def b_to_sbuf(c):
+            b_rows[c] = rows2.tile([P, CHUNK_COLS], F32, name="b_rows", tag="b_rows")
+            nc.scalar.copy(out=b_rows[c][:], in_=z_b[c][:].rearrange("p t r -> p (t r)"))
+
+        def add_b_on_tensor(c):
+            sums[c] = bank_tile([P, CHUNK_COLS], 0)
+            nc.tensor.matmul(out=sums[c][:], lhsT=ident[:], rhs=parts[c][:, 0], start=True, stop=False)
+            nc.tensor.matmul(out=sums[c][:], lhsT=ident[:], rhs=b_rows[c][:], start=False, stop=True)
+
+        def store_sum(c):
+            t0 = c * CHUNK_TILES
+            nc.scalar.copy(out=parts[c][:, 0], in_=sums[c][:])
+            nc.sync.dma_start(out=re_rows[:, t0 : t0 + CHUNK_TILES, :], in_=parts[c][:, 0].rearrange("p (t r) -> p t r", r=R))
 
         def add_b(c):
             t0 = c * CHUNK_TILES
@@ -414,7 +488,7 @@ def tile_mamba3mimoblock_pa_kernel(
 
         def damp_and_store(c):
             t0 = c * CHUNK_TILES
-            decay_t = None if c in damped else back_to_rows(soft[c], "D%d" % c)
+            decay_t = None if c in damped else back_to_rows(decays[c], "D%d" % c)
             if c in damped:
                 pass
             elif c in G_DAMP:
@@ -429,8 +503,7 @@ def tile_mamba3mimoblock_pa_kernel(
             nc.sync.dma_start(out=re_rows[:, t0 : t0 + CHUNK_TILES, :], in_=parts[c][:, 0].rearrange("p (t r) -> p t r", r=R))
 
         steps = {
-            "EX": exp_of, "TH": tanh_of, "CAP": cap, "LN": logarithm, "ST": step_size, "U": angle, "RN": nearest_even,
-            "FR": fraction, "SN": sine_of, "DI": damp_im, "DR": damp_re, "DB": damp_both, "BA": add_b, "HF": halve_tanh, "RG": nearest_turn, "FG": fraction_g, "FV": fraction_v, "HV": halve_tanh_v, "TT": silu_table, "AB": magnitude_of, "CS": cosine_of, "DC": decay, "BV": b_val, "RS": rot_sin, "RC": rot_cos, "RA": rot_add, "DS": damp_state,
+            "EX": exp_of, "UP": angle_pair, "UG": angle_on_gpsimd, "RP": nearest_pair, "CP": cap_pair, "LP": log_pair, "DP": decay_pair_of, "TH": tanh_of, "CAP": cap, "LN": logarithm, "ST": step_size, "U": angle,             "SN": sine_of, "DI": damp_im, "DR": damp_re, "DB": damp_both, "BA": add_b, "RV": turned_re_on_vector, "RI": turned_im, "ZC": b_to_sbuf, "PB": add_b_on_tensor, "SO": store_sum, "HF": halve_tanh, "RG": nearest_turn, "FG": fraction_g, "FV": fraction_v, "HV": halve_tanh_v, "TT": silu_table, "AB": magnitude_of, "CS": cosine_of, "DC": decay, "BV": b_val, "RS": rot_sin, "RC": rot_cos, "RA": rot_add, "DS": damp_state, "DX": lambda c: damp_state_half(c, 0), "DY": lambda c: damp_state_half(c, 1),
             "DMP": damp_and_store,
         }
 

import math
from contextlib import ExitStack

import concourse.mybir as mybir
from concourse.masks import make_identity

F32 = mybir.dt.float32
BF16 = mybir.dt.bfloat16
U32 = mybir.dt.uint32
U8 = mybir.dt.uint8
I32 = mybir.dt.int32
FP8X4 = mybir.dt.float8_e4m3fn_x4
ACT = mybir.ActivationFunctionType
ALU = mybir.AluOpType

B, D, R = 2048, 2048, 128
FLOPS = 2 * B * D * 3 * R

P = 128
PACK = 4
K_PASS = P * PACK
PASSES = D // K_PASS
WORDS_PASS = K_PASS // 2

ROW_TILES = B // P
PIECE_TILES = 2
PIECES = ROW_TILES // PIECE_TILES
PIECE_COLS = PIECE_TILES * P
CHUNK_TILES = 4
CHUNK_COLS = CHUNK_TILES * P
CHUNKS = ROW_TILES // CHUNK_TILES
PIECES_PER_CHUNK = CHUNK_TILES // PIECE_TILES

X_BUFFERS = 6
PRODUCT_LAG = 1
EXP_CAP = 2.0**60

CFG = {"plan": {"0,4": "Q0","1,1": "VA0","1,4": "MD0 Q1","2,0": "MP0","2,4": "Q2","3,0": "M1","3,2": "EX0 TH0 HF0","3,4": "Q3 CAP0","4,0": "M2","4,4": "Q4","5,0": "M3","5,2": "EX1 TH1 HF1","5,4": "CAP1 Q5 LN0 LN1","6,0": "MP4","6,3": "MD5 ST0 ST1 U0 RG0","6,4": "Q6","7,0": "MP5 FG0","7,1": "EX2 TH2 HF2","7,2": "","7,3": "CAP2","7,4": "Q7 U1","8,0": "M6 WB0 M7 DC0 DC1 RG1 FG1 EX3 TH3 HF3 CAP3 LN2 LN3 DS0 DS1 BV0 BV1 BV2 BV3 ST2 ST3 U2 U3 RG2 RG3 FG2 FG3 SN0 AB0 CS0 SN1 AB1 CS1 RS0 RC0 RA0 RS1 RC1 RA1 SN2 AB2 CS2 SN3 AB3 CS3 RS2 RC2 RI2 RS3 RC3 DI0 DI1 RV2 RA3 DC2 DC3 DB2 BA0 BA2 DR3 DI3 BA1 BA3","2,1": "VEC VS3","1,3": "VS2","3,1": "VS4","4,1": "VS5","5,3": "MD4"},"sb": {"0": [1,3],"1": [1,2],"2": [0,1,2],"3": [0,1,2],"4": [0,1,2],"5": [0],"6": [0,1,2,3],"7": [0]},"wb": [[],[0,2]],"xt": [0,1,2,3],"zdt": [4,6,7,4],"zph": [5,5,5,5],"rowb": {"B0": 6,"B1": 0,"S0": 1,"C0": 2,"S1": 3,"C1": 7,"S2": 5,"C2": 4,"S3": 1,"C3": 2,"D0": 3,"D1": 7,"D2": 5,"D3": 4,"B2": 6,"B3": 0},"sort": [3],"gdamp": [],"cap": "vector","wdt_cuts": [[0,1024],[1024,2048]],"x0_cuts": [[0,1024],[1024,2048]],"wb_after": 7,"vadd": [],"cb": [0,1],"first_w": [0,1],"loads": [["w",0,0,2],["w",0,1,2],["w",1,0,1],["x",0,0,2],["x",0,1,2],["x",1,0,2],["x",1,1,2],["x",2,0,1],["x",3,0,1],["x",4,0,1],["x",5,0,1],["x",6,0,1],["x",7,0,1],["w",2,0,1]],"sortp": [[],[],[],[],[],[],[],[]],"vs": {"2": [[3,"v"],[2,"v"],[1,"s"]],"3": [[3,"v"],[2,"v"],[1,"s"]],"4": [[3,"v"],[2,"v"],[1,"s"]],"5": [[3,"v"],[2,"v"],[1,"s"]]},"unit": 2}
PLAN = {tuple(int(v) for v in k.split(",")): v.split() for k, v in CFG["plan"].items()}
SCALAR_BANKS = {int(k): tuple(v) for k, v in CFG["sb"].items()}
W_BANKS = tuple(CFG["wb"])
X_BUFFERS = 5
ROUND_MAGIC = 1.5 * 2.0**23
UNIT = CFG.get("unit", 1.0)
WB_SLOT = 7
BANKS = 8
XT = tuple(CFG["xt"])
ZDT = tuple(CFG["zdt"])
ZPH = tuple(CFG["zph"])
ROWB = CFG["rowb"]
SORTED_PASSES = tuple(CFG["sort"])
VEC_SLOT = 1
CAP_ENGINE = CFG["cap"]
G_DAMP = tuple(CFG['gdamp'])


def tile_mamba3mimoblock_pa_kernel(
    tc, x, state_re, state_im, W_dt, b_dt, W_ph, b_ph, W_B, A_real, A_imag, out_0, out_1
):
    nc = tc.nc
    with ExitStack() as ctx:
        const = ctx.enter_context(tc.tile_pool(name="const", bufs=1))
        xpool = ctx.enter_context(tc.tile_pool(name="xpool", bufs=X_BUFFERS))
        stage = ctx.enter_context(tc.tile_pool(name="stage", bufs=3))
        keep = ctx.enter_context(tc.tile_pool(name="keep", bufs=1))
        chan2 = ctx.enter_context(tc.tile_pool(name="chan2", bufs=2))
        chan3 = ctx.enter_context(tc.tile_pool(name="chan3", bufs=3))
        rows = ctx.enter_context(tc.tile_pool(name="rows", bufs=CHUNKS))
        rows3 = ctx.enter_context(tc.tile_pool(name="rows3", bufs=3))
        rows2 = ctx.enter_context(tc.tile_pool(name="rows2", bufs=2))
        psum = ctx.enter_context(tc.psum_pool(name="psum", bufs=8))
        xt_count = [0]

        def bank_tile(shape, which):
            bank = psum.tile(shape, F32, name="bank", tag="bank")
            return bank

        def next_xt(shape):
            xt_count[0] += 1
            return bank_tile(shape, XT[(xt_count[0] - 1) % len(XT)])

        ctx.enter_context(tc.manual_schedule())

        x_rows = x.rearrange("(p t) k -> p t k", t=ROW_TILES)
        re_rows = out_0.rearrange("(p t) r -> p t r", t=ROW_TILES)
        im_rows = out_1.rearrange("(p t) r -> p t r", t=ROW_TILES)

        vec_rows = const.tile([P, P], BF16)
        nc.vector.memset(vec_rows[:], 0.0)
        for i, vec in enumerate((b_dt, b_ph, A_real, A_imag)):
            nc.scalar.dma_start(out=vec_rows[i : i + 1, :], in_=vec.rearrange("(o r) -> o r", o=1))

        w_sb = const.tile([P, 3, D], BF16)
        x_sb = {}

        def load_weight(i, part, parts_of):
            k0, k1 = part * D // parts_of, (part + 1) * D // parts_of
            nc.sync.dma_start(out=w_sb[:, i, k0:k1], in_=(W_dt, W_ph, W_B)[i][:, k0:k1])

        def load_x(piece, part, parts_of):
            if part == 0:
                x_sb[piece] = xpool.tile([P, parts_of, PIECE_TILES, D // parts_of], BF16, name="x_piece", tag="x_piece")
            k0, k1 = part * D // parts_of, (part + 1) * D // parts_of
            t0 = piece * PIECE_TILES
            nc.sync.dma_start(out=x_sb[piece][:, part], in_=x_rows[:, t0 : t0 + PIECE_TILES, k0:k1])

        for kind, i, part, parts_of in CFG["loads"]:
            if kind == "w":
                load_weight(i, part, parts_of)
            else:
                load_x(i, part, parts_of)
        state = const.tile([P, 2, ROW_TILES, R], BF16)
        nc.sync.dma_start(out=state[:, 0], in_=state_re.rearrange("(p t) r -> p t r", t=ROW_TILES))
        nc.sync.dma_start(out=state[:, 1], in_=state_im.rearrange("(p t) r -> p t r", t=ROW_TILES))

        ident = const.tile([P, P], F32)
        make_identity(nc, ident[:])

        def transposes_and_copies(words, n_tiles, scalar_banks, presorted=None, slot=None):
            out_tile = stage.tile([P, PASSES * n_tiles * P * PACK], BF16, name="grouped", tag="grouped", align_bytes=64)
            if slot is not None:
                grouped[slot] = out_tile
            grouped_words = out_tile[:].bitcast(F32).rearrange("q (g c u) -> q g c u", g=PASSES, u=2)
            for g in range(PASSES):
                bank = next_xt([P, 2, n_tiles, P])
                pass_words = pass_of(slot, g) if slot is not None else words[:, :, g * WORDS_PASS : (g + 1) * WORDS_PASS]
                for u in range(2):
                    for j in range(n_tiles):
                        chosen = presorted[g][:, j, u, :] if presorted and g in presorted else pass_words[:, j, u:WORDS_PASS:2]
                        nc.tensor.transpose(bank[:, u, j, :], chosen, ident[:])
                halves = bank[:].rearrange("q u j p -> q (j p) u")
                if g in scalar_banks:
                    nc.scalar.copy(out=grouped_words[:, g], in_=halves)
                else:
                    nc.vector.tensor_copy(out=grouped_words[:, g], in_=halves)
                if slot is not None:
                    follow(slot, g)
            return out_tile

        w_words = w_sb[:].bitcast(F32)
        w2_codes = keep.tile([P, 2, PASSES, P], U32, align_bytes=64)
        w2_scales = keep.tile([P, 2, PASSES, P], U8, align_bytes=64)
        wb_codes = keep.tile([P, PASSES, P], U32, align_bytes=64)
        wb_scales = keep.tile([P, PASSES, P], U8, align_bytes=64)
        def weights_a(i):
            w2_grouped = transposes_and_copies(w_words[:, i : i + 1, :], 1, W_BANKS[i])
            nc.vector.quantize_mx(
                out=w2_codes[:, i].rearrange("q g r -> q (g r)").bitcast(FP8X4),
                scales=w2_scales[:, i].rearrange("q g r -> q (g r)"),
                in_=w2_grouped[:],
            )

        cols = {}

        def vec_copy(c):
            cols["vec"] = const.tile([P, P], F32, name="vec_f32")
            nc.vector.tensor_copy(out=cols["vec"][:], in_=vec_rows[:])

        def channel_constants():
            vec_f32 = cols["vec"]
            vec_t = bank_tile([P, P], 7)
            nc.tensor.transpose(vec_t[:], vec_f32[:], ident[:])
            per_chan = const.tile([P, 4], F32, name="per_chan")
            nc.vector.tensor_copy(out=per_chan[:], in_=vec_t[:, 0:4])
            cols["b_dt"] = per_chan[:, 0:1]
            cols["b_ph"] = per_chan[:, 1:2]
            a_col = const.tile([P, 1], F32, name="a_col")
            nc.scalar.activation(out=a_col[:], in_=per_chan[:, 2:3], func=ACT.Exp)
            neg_a_col = const.tile([P, 1], F32, name="neg_a_col")
            nc.gpsimd.tensor_scalar(out=neg_a_col[:], in0=a_col[:], scalar1=-1.0, scalar2=0.0, op0=ALU.mult, op1=ALU.add)
            cols["neg_a"] = neg_a_col[:]
            half_turns_col = const.tile([P, 1], F32, name="half_turns_col")
            nc.vector.tensor_scalar_mul(out=half_turns_col[:], in0=per_chan[:, 3:4], scalar1=1.0 / (math.pi * UNIT))
            cols["half_turns"] = half_turns_col[:]
            cols["scratch"] = const.tile([P, 1], F32, name="scratch")[:]

        grouped = {}
        x_codes = keep.tile([P, PIECES, PASSES, PIECE_TILES, P], U32, align_bytes=64)
        x_scales = keep.tile([P, PIECES, PASSES, PIECE_TILES, P], U8, align_bytes=64)
        soft_pair, turn_pair, turns_pair, decay_tile = {}, {}, {}, {}
        turns, z_dt, z_ph, z_b, soft, turn, frac, sine, cosine, parts = {}, {}, {}, {}, {}, {}, {}, {}, {}, {}

        def pass_of(piece, g):
            words = x_sb[piece][:].bitcast(F32)
            per_cut = PASSES // words.shape[1]
            return words[:, g // per_cut, :, (g % per_cut) * WORDS_PASS : (g % per_cut + 1) * WORDS_PASS]

        def sort_words(piece):
            out = {}
            for g in (CFG['sortp'][piece] if 'sortp' in CFG else SORTED_PASSES):
                by_parity = stage.tile([P, PIECE_TILES, 2, P], F32, name="by_parity", tag="by_parity", bufs=6)
                pass_words = pass_of(piece, g)
                nc.gpsimd.tensor_copy(out=by_parity[:], in_=pass_words.rearrange("p j (q u) -> p j u q", u=2))
                out[g] = by_parity
            return out

        def vector_sort(piece):
            if CFG.get("merge") and len(CFG["vs"][str(piece)]) == 2:
                by_parity = stage.tile([P, 2, PIECE_TILES, 2, P], F32, name="by_parity2", tag="by_parity2", bufs=3)
                words = x_sb[piece][:].bitcast(F32)[:, 0, :, 2 * WORDS_PASS : 4 * WORDS_PASS]
                nc.vector.tensor_copy(out=by_parity[:], in_=words.rearrange("p j (g q u) -> p g j u q", g=2, u=2))
                sorted_words.setdefault(piece, {}).update({2: by_parity[:, 0], 3: by_parity[:, 1]})
                return
            for g, eng in CFG["vs"][str(piece)]:
                by_parity = stage.tile([P, PIECE_TILES, 2, P], F32, name="by_parity", tag="by_parity", bufs=6)
                src = pass_of(piece, g).rearrange("p j (q u) -> p j u q", u=2)
                if eng == "v":
                    nc.vector.tensor_copy(out=by_parity[:], in_=src)
                else:
                    nc.scalar.copy(out=by_parity[:], in_=src)
                sorted_words.setdefault(piece, {})[g] = by_parity

        def quantise(piece, grouped):
            nc.vector.quantize_mx(
                out=x_codes[:, piece].rearrange("q g j p -> q (g j p)").bitcast(FP8X4),
                scales=x_scales[:, piece].rearrange("q g j p -> q (g j p)"),
                in_=grouped[:],
            )

        def quantise_half(piece, half):
            cut = PASSES // 2
            width = PASSES * PIECE_TILES * P * PACK // 2
            nc.vector.quantize_mx(
                out=x_codes[:, piece, half * cut : (half + 1) * cut].rearrange("q g j p -> q (g j p)").bitcast(FP8X4),
                scales=x_scales[:, piece, half * cut : (half + 1) * cut].rearrange("q g j p -> q (g j p)"),
                in_=grouped[piece][:, half * width : (half + 1) * width],
            )

        def products_half(piece, passes):
            c = piece // PIECES_PER_CHUNK
            half = piece % PIECES_PER_CHUNK
            if c not in z_dt:
                z_dt[c] = bank_tile([P, CHUNK_COLS], 0)
                z_ph[c] = bank_tile([P, CHUNK_COLS], 0)
            cols_ = slice(half * PIECE_COLS, (half + 1) * PIECE_COLS)
            for g in passes:
                for i, z in enumerate((z_dt[c], z_ph[c])):
                    nc.tensor.matmul_mx(
                        out=z[:, cols_],
                        lhsT=w2_codes[:, i, g, :].bitcast(FP8X4),
                        lhsT_scale=w2_scales[:, i, g, :],
                        rhs=x_codes[:, piece, g].rearrange("q j p -> q (j p)").bitcast(FP8X4),
                        rhs_scale=x_scales[:, piece, g].rearrange("q j p -> q (j p)"),
                        start=(g == 0),
                        stop=(g == PASSES - 1),
                    )

        def products(piece, which=(0, 1)):
            c = piece // PIECES_PER_CHUNK
            half = piece % PIECES_PER_CHUNK
            if half == 0 and c not in z_dt:
                z_dt[c] = bank_tile([P, CHUNK_COLS], ZDT[c])
                z_ph[c] = bank_tile([P, CHUNK_COLS], ZPH[c])
            cols = slice(half * PIECE_COLS, (half + 1) * PIECE_COLS)
            for i in which:
                z = (z_dt[c], z_ph[c])[i]
                for g in range(PASSES):
                    nc.tensor.matmul_mx(
                        out=z[:, cols],
                        lhsT=w2_codes[:, i, g, :].bitcast(FP8X4),
                        lhsT_scale=w2_scales[:, i, g, :],
                        rhs=x_codes[:, piece, g].rearrange("q j p -> q (j p)").bitcast(FP8X4),
                        rhs_scale=x_scales[:, piece, g].rearrange("q j p -> q (j p)"),
                        start=(g == 0),
                        stop=(g == PASSES - 1),
                    )

        def exp_of(c):
            if c % 2 == 0:
                soft_pair[c // 2] = chan2.tile([P, 2, CHUNK_COLS], F32, name="soft", tag="soft")
            soft[c] = soft_pair[c // 2][:, c % 2]
            nc.scalar.activation(out=soft[c], in_=z_dt[c][:], func=ACT.Exp, bias=cols["b_dt"], scale=1.0)

        def tanh_of(c):
            if c % 2 == 0:
                turn_pair[c // 2] = chan2.tile([P, 2, CHUNK_COLS], F32, name="turn", tag="turn")
            turn[c] = turn_pair[c // 2][:, c % 2]
            nc.scalar.activation(out=turn[c], in_=z_ph[c][:], func=ACT.Tanh, bias=cols["b_ph"], scale=1.0)

        def cap(c):
            if CAP_ENGINE == "gpsimd":
                nc.gpsimd.tensor_scalar(
                    out=soft[c], in0=soft[c], scalar1=EXP_CAP, scalar2=1.0, op0=ALU.min, op1=ALU.add
                )
            else:
                nc.vector.tensor_scalar(
                    out=soft[c], in0=soft[c], scalar1=EXP_CAP, scalar2=1.0, op0=ALU.min, op1=ALU.add
                )

        def b_val(c):
            z_b[c] = bank_tile([P, CHUNK_TILES, R], ROWB["B%d" % c])
            for jj in range(CHUNK_TILES):
                piece = (c * CHUNK_TILES + jj) // PIECE_TILES
                j = (c * CHUNK_TILES + jj) % PIECE_TILES
                for g in range(PASSES):
                    nc.tensor.matmul_mx(
                        out=z_b[c][:, jj, :],
                        lhsT=x_codes[:, piece, g, j, :].bitcast(FP8X4),
                        lhsT_scale=x_scales[:, piece, g, j, :],
                        rhs=wb_codes[:, g, :].bitcast(FP8X4),
                        rhs_scale=wb_scales[:, g, :],
                        start=(g == 0),
                        stop=(g == PASSES - 1),
                    )

        def logarithm(c):
            nc.scalar.activation(out=soft[c], in_=soft[c], func=ACT.Ln)

        def step_size(c):
            nc.vector.scalar_tensor_tensor(
                out=soft[c], in0=z_dt[c][:], scalar=cols["b_dt"], in1=soft[c], op0=ALU.add, op1=ALU.max
            )

        def angle(c):
            nc.vector.scalar_tensor_tensor(
                out=turn[c], in0=soft[c], scalar=cols["half_turns"], in1=turn[c], op0=ALU.mult, op1=ALU.add
            )

        def halve_tanh(c):
            nc.gpsimd.tensor_scalar(
                out=turn[c], in0=turn[c], scalar1=0.5, scalar2=0.0, op0=ALU.mult, op1=ALU.add
            )

        def nearest_turn(c):
            if c % 2 == 0:
                turns_pair[c // 2] = chan2.tile([P, 2, CHUNK_COLS], F32, name="turns", tag="turns")
            turns[c] = turns_pair[c // 2][:, c % 2]
            nc.vector.tensor_scalar(
                out=turns[c], in0=turn[c], scalar1=ROUND_MAGIC, scalar2=ROUND_MAGIC, op0=ALU.add, op1=ALU.subtract
            )

        def fraction_g(c):
            frac[c] = turn[c]
            nc.gpsimd.tensor_sub(out=frac[c], in0=turns[c], in1=turn[c])

        def fraction_v(c):
            frac[c] = turn[c]
            nc.vector.tensor_sub(out=frac[c], in0=turns[c], in1=turn[c])

        def halve_tanh_v(c):
            nc.vector.tensor_scalar_mul(out=turn[c], in0=turn[c], scalar1=0.5)

        def silu_table(c):
            nc.scalar.activation(out=cols["scratch"], in_=cols["b_dt"], func=ACT.Silu)

        def sine_of(c):
            sine[c] = chan3.tile([P, CHUNK_COLS], F32, name="sine", tag="sine")
            nc.scalar.activation(out=sine[c][:], in_=frac[c], func=ACT.Sin, scale=-math.pi * UNIT)

        def magnitude_of(c):
            cosine[c] = chan3.tile([P, CHUNK_COLS], F32, name="cosine", tag="cosine")
            nc.scalar.activation(out=cosine[c][:], in_=frac[c], func=ACT.Abs)

        def cosine_of(c):
            nc.scalar.activation(
                out=cosine[c][:], in_=cosine[c][:], func=ACT.Sin, scale=-math.pi * UNIT, bias=math.pi / 2.0
            )

        decays = {}

        def decay_pair_of(h):
            both_chunks = chan2.tile([P, 2, CHUNK_COLS], F32, name="decay", tag="decay")
            nc.scalar.activation(out=both_chunks[:], in_=soft_pair[h][:], func=ACT.Exp, scale=cols["neg_a"])
            for i in range(2):
                decays[2 * h + i] = both_chunks[:, i]

        def decay(c):
            if c % 2 == 0:
                decay_tile[c // 2] = chan2.tile([P, 2, CHUNK_COLS], F32, name="decay", tag="decay")
            decays[c] = decay_tile[c // 2][:, c % 2]
            nc.scalar.activation(out=decays[c], in_=soft[c], func=ACT.Exp, scale=cols["neg_a"])

        def angle_on_gpsimd(c):
            product = chan3.tile([P, CHUNK_COLS], F32, name="product", tag="product")
            nc.gpsimd.tensor_scalar(
                out=product[:], in0=soft[c], scalar1=cols["half_turns"], scalar2=0.0, op0=ALU.mult, op1=ALU.add
            )
            nc.gpsimd.tensor_add(out=turn[c], in0=product[:], in1=turn[c])

        def angle_pair(h):
            nc.vector.scalar_tensor_tensor(
                out=turn_pair[h][:], in0=soft_pair[h][:], scalar=cols["half_turns"], in1=turn_pair[h][:], op0=ALU.mult, op1=ALU.add
            )

        def nearest_pair(h):
            turns_pair[h] = chan2.tile([P, 2, CHUNK_COLS], F32, name="turns", tag="turns")
            nc.vector.tensor_scalar(
                out=turns_pair[h][:], in0=turn_pair[h][:], scalar1=ROUND_MAGIC, scalar2=ROUND_MAGIC, op0=ALU.add, op1=ALU.subtract
            )
            for i in range(2):
                turns[2 * h + i] = turns_pair[h][:, i]

        def cap_pair(h):
            nc.vector.tensor_scalar(
                out=soft_pair[h][:], in0=soft_pair[h][:], scalar1=EXP_CAP, scalar2=1.0, op0=ALU.min, op1=ALU.add
            )

        def log_pair(h):
            nc.scalar.activation(out=soft_pair[h][:], in_=soft_pair[h][:], func=ACT.Ln)

        def back_to_rows(channel_tile, which):
            bank = bank_tile([P, CHUNK_TILES, R], ROWB[which])
            for jj in range(CHUNK_TILES):
                nc.tensor.transpose(bank[:, jj, :], channel_tile[:, jj * P : (jj + 1) * P], ident[:])
            return bank

        def both(bank):
            return bank[:].rearrange("p t r -> p (t r)").unsqueeze(1).broadcast_to([P, 2, CHUNK_COLS])

        by_sin, by_cos, damped, decay_banks = {}, {}, {}, {}

        def damp_state_half(c, i):
            t0 = c * CHUNK_TILES
            if i == 0:
                damped[c] = rows2.tile([P, 2, CHUNK_COLS], F32, name="damped", tag="damped")
                decay_banks[c] = back_to_rows(decays[c], "D%d" % c)
            st = state[:, i, t0 : t0 + CHUNK_TILES, :].rearrange("p t r -> p (t r)")
            nc.vector.tensor_mul(out=damped[c][:, i], in0=st, in1=decay_banks[c][:].rearrange("p t r -> p (t r)"))

        def damp_state(c):
            t0 = c * CHUNK_TILES
            st = state[:, :, t0 : t0 + CHUNK_TILES, :].rearrange("p c t r -> p c (t r)")
            damped[c] = rows2.tile([P, 2, CHUNK_COLS], F32, name="damped", tag="damped")
            nc.vector.tensor_mul(out=damped[c][:], in0=st, in1=both(back_to_rows(decays[c], "D%d" % c)))

        def rot_sin(c):
            t0 = c * CHUNK_TILES
            st = damped[c][:] if c in damped else state[:, :, t0 : t0 + CHUNK_TILES, :].rearrange("p c t r -> p c (t r)")
            by_sin[c] = rows3.tile([P, 2, CHUNK_COLS], F32, name="by_sin", tag="by_sin")
            nc.vector.tensor_mul(out=by_sin[c][:], in0=st, in1=both(back_to_rows(sine[c], "S%d" % c)))

        def rot_cos(c):
            t0 = c * CHUNK_TILES
            st = damped[c][:] if c in damped else state[:, :, t0 : t0 + CHUNK_TILES, :].rearrange("p c t r -> p c (t r)")
            by_cos[c] = rows.tile([P, 2, CHUNK_COLS], F32, name="by_cos", tag="by_cos")
            nc.vector.tensor_mul(out=by_cos[c][:], in0=st, in1=both(back_to_rows(cosine[c], "C%d" % c)))

        def rot_add(c):
            parts[c] = by_cos[c]
            eng = nc.vector if c in CFG["vadd"] else nc.gpsimd
            eng.tensor_sub(out=parts[c][:, 0], in0=by_cos[c][:, 0], in1=by_sin[c][:, 1])
            eng.tensor_add(out=parts[c][:, 1], in0=by_cos[c][:, 1], in1=by_sin[c][:, 0])

        def turned_re_on_vector(c):
            parts[c] = by_cos[c]
            nc.vector.tensor_sub(out=parts[c][:, 0], in0=by_cos[c][:, 0], in1=by_sin[c][:, 1])

        def turned_im(c):
            parts[c] = by_cos[c]
            nc.gpsimd.tensor_add(out=parts[c][:, 1], in0=by_cos[c][:, 1], in1=by_sin[c][:, 0])

        def damp_im(c):
            t0 = c * CHUNK_TILES
            if c not in damped:
                nc.vector.tensor_mul(out=parts[c][:, 1], in0=parts[c][:, 1], in1=decay_banks[c][:].rearrange("p t r -> p (t r)"))
            nc.sync.dma_start(out=im_rows[:, t0 : t0 + CHUNK_TILES, :], in_=parts[c][:, 1].rearrange("p (t r) -> p t r", r=R))

        def damp_re(c):
            decay_banks[c] = back_to_rows(decays[c], "D%d" % c)
            nc.vector.tensor_mul(out=parts[c][:, 0], in0=parts[c][:, 0], in1=decay_banks[c][:].rearrange("p t r -> p (t r)"))

        def damp_both(c):
            t0 = c * CHUNK_TILES
            decay_banks[c] = back_to_rows(decays[c], "D%d" % c)
            nc.vector.tensor_mul(out=parts[c][:], in0=parts[c][:], in1=both(decay_banks[c]))
            nc.sync.dma_start(out=im_rows[:, t0 : t0 + CHUNK_TILES, :], in_=parts[c][:, 1].rearrange("p (t r) -> p t r", r=R))

        b_rows, sums = {}, {}

        def b_to_sbuf(c):
            b_rows[c] = rows2.tile([P, CHUNK_COLS], F32, name="b_rows", tag="b_rows")
            nc.scalar.copy(out=b_rows[c][:], in_=z_b[c][:].rearrange("p t r -> p (t r)"))

        def add_b_on_tensor(c):
            sums[c] = bank_tile([P, CHUNK_COLS], 0)
            nc.tensor.matmul(out=sums[c][:], lhsT=ident[:], rhs=parts[c][:, 0], start=True, stop=False)
            nc.tensor.matmul(out=sums[c][:], lhsT=ident[:], rhs=b_rows[c][:], start=False, stop=True)

        def store_sum(c):
            t0 = c * CHUNK_TILES
            nc.scalar.copy(out=parts[c][:, 0], in_=sums[c][:])
            nc.sync.dma_start(out=re_rows[:, t0 : t0 + CHUNK_TILES, :], in_=parts[c][:, 0].rearrange("p (t r) -> p t r", r=R))

        def add_b(c):
            t0 = c * CHUNK_TILES
            nc.vector.tensor_add(out=parts[c][:, 0], in0=parts[c][:, 0], in1=z_b[c][:].rearrange("p t r -> p (t r)"))
            nc.sync.dma_start(out=re_rows[:, t0 : t0 + CHUNK_TILES, :], in_=parts[c][:, 0].rearrange("p (t r) -> p t r", r=R))

        def damp_and_store(c):
            t0 = c * CHUNK_TILES
            decay_t = None if c in damped else back_to_rows(decays[c], "D%d" % c)
            if c in damped:
                pass
            elif c in G_DAMP:
                decay_rows = rows.tile([P, CHUNK_COLS], F32, name="decay_rows", tag="decay_rows")
                nc.scalar.copy(out=decay_rows[:], in_=decay_t[:].rearrange("p t r -> p (t r)"))
                for i in range(2):
                    nc.gpsimd.tensor_mul(out=parts[c][:, i], in0=parts[c][:, i], in1=decay_rows[:])
            else:
                nc.vector.tensor_mul(out=parts[c][:], in0=parts[c][:], in1=both(decay_t))
            nc.sync.dma_start(out=im_rows[:, t0 : t0 + CHUNK_TILES, :], in_=parts[c][:, 1].rearrange("p (t r) -> p t r", r=R))
            nc.vector.tensor_add(out=parts[c][:, 0], in0=parts[c][:, 0], in1=z_b[c][:].rearrange("p t r -> p (t r)"))
            nc.sync.dma_start(out=re_rows[:, t0 : t0 + CHUNK_TILES, :], in_=parts[c][:, 0].rearrange("p (t r) -> p t r", r=R))

        steps = {
            "EX": exp_of, "UP": angle_pair, "UG": angle_on_gpsimd, "RP": nearest_pair, "CP": cap_pair, "LP": log_pair, "DP": decay_pair_of, "TH": tanh_of, "CAP": cap, "LN": logarithm, "ST": step_size, "U": angle,             "SN": sine_of, "DI": damp_im, "DR": damp_re, "DB": damp_both, "BA": add_b, "RV": turned_re_on_vector, "RI": turned_im, "ZC": b_to_sbuf, "PB": add_b_on_tensor, "SO": store_sum, "HF": halve_tanh, "RG": nearest_turn, "FG": fraction_g, "FV": fraction_v, "HV": halve_tanh_v, "TT": silu_table, "AB": magnitude_of, "CS": cosine_of, "DC": decay, "BV": b_val, "RS": rot_sin, "RC": rot_cos, "RA": rot_add, "DS": damp_state, "DX": lambda c: damp_state_half(c, 0), "DY": lambda c: damp_state_half(c, 1),
            "DMP": damp_and_store,
        }

        sorted_words = {}
        steps["M"] = products
        steps["VS"] = vector_sort
        steps["MA"] = lambda c: products_half(c, (0, 1))
        steps["MZ"] = lambda c: products_half(c, (2, 3))
        steps["MD"] = lambda c: products(c, (0,))
        steps["MP"] = lambda c: products(c, (1,))
        steps["QA"] = lambda c: quantise_half(c, 0)
        steps["QZ"] = lambda c: quantise_half(c, 1)
        steps["Q"] = lambda c: quantise(c, grouped[c])
        def weights_b(c):
            wb_grouped = transposes_and_copies(w_words[:, 2:3, :], 1, tuple(CFG.get("cb", (0, 2))))
            nc.vector.quantize_mx(
                out=wb_codes[:].rearrange("q g r -> q (g r)").bitcast(FP8X4),
                scales=wb_scales[:].rearrange("q g r -> q (g r)"),
                in_=wb_grouped[:],
            )
        steps["WB"] = weights_b
        steps["W"] = weights_a
        for i in CFG["first_w"]:
            weights_a(i)

        def follow(slot, g):
            for step in PLAN.get((slot, g), []):
                if step == "VA0":
                    vec_copy(0)
                elif step == "VEC":
                    channel_constants()
                else:
                    steps[step[:-1]](int(step[-1:]))

        sorted_words[0] = sort_words(0)
        for piece in range(PIECES):
            if piece + 1 < PIECES:
                sorted_words.setdefault(piece + 1, {}).update(sort_words(piece + 1))
            transposes_and_copies(None, PIECE_TILES, SCALAR_BANKS[piece], sorted_words[piece], piece)
            follow(piece, 4)
        follow(PIECES, 0)
